import numpy as np
import ml_dtypes


def mxq(x, axis, fmt="e4m3"):
    dtype, down = {"e4m3": (ml_dtypes.float8_e4m3fn, 7), "e5m2": (ml_dtypes.float8_e5m2, 14)}[fmt]
    v = np.moveaxis(np.asarray(x, np.float32).astype(ml_dtypes.bfloat16).astype(np.float64), axis, -1)
    blocks = v.reshape(v.shape[:-1] + (-1, 32))
    amax = np.abs(blocks).max(-1, keepdims=True)
    byte = np.maximum(np.where(amax > 0, np.frexp(amax)[1] - 1 + 127, 0) - down, 1)
    scale = np.exp2(byte - 127.0)
    codes = (blocks / scale).astype(np.float32).astype(dtype).astype(np.float64)
    return np.moveaxis((codes * scale).reshape(v.shape), -1, axis)


WIDE = False


def mx_kscale(k):
    if not WIDE:
        return np.ones(k)
    levels = np.array([10, -10, 5, -5, 0])
    if k % 512:
        return np.exp2(np.random.permutation(np.resize(levels, k // 32))).repeat(32)
    a = np.empty((k // 512, 16))
    for p in range(k // 512):
        a[p, :8] = np.random.permutation(np.resize(levels, 8))
        for g in range(8):
            far = levels[np.abs(levels - a[p, g]) >= 10]
            a[p, g + 8] = far[np.random.randint(len(far))]
    return np.exp2(a.ravel()).repeat(32)


BF16 = ml_dtypes.bfloat16


def bf(x):
    return np.asarray(x, np.float32).astype(BF16)


def f64(x):
    return np.asarray(x).astype(np.float64)


B, D_IN, D_H, C = 8192, 512, 512, 128
TAU, T1, T2 = 0.5, 3, 3
G, GB = 3.0, 3.0


def inv_apprx(v, t, m):
    a = 2.0 - (2.0 / m) * v
    b = 1.0 - (2.0 / m) * v
    for _ in range(t):
        b = b * b
        a = a * (1.0 + b)
    return (2.0 / m) * a


def comp_max_tau(p, tau, t1, t2):
    res = np.concatenate([p, np.full((p.shape[0], 1), tau)], axis=1)
    for i in range(t1):
        res = res * res
        sum_res = res.sum(axis=1)
        m = (2.0 + tau * tau) if i == 0 else 2.0
        res = res * inv_apprx(sum_res, t2, m)[:, None]
    return res[:, -1]


def softmax(z):
    e = np.exp(z - z.max(-1, keepdims=True))
    return e / e.sum(-1, keepdims=True)


def mlp(xq, W1, b1, W2, b2):
    h = np.maximum((xq @ mxq(f64(W1), 0, "e4m3")) + f64(b1), 0.0)
    return softmax((mxq(h, 1, "e4m3") @ mxq(f64(W2), 0, "e4m3")) + f64(b2))


def setup_inputs():
    s, t = mx_kscale(D_IN), mx_kscale(D_H)
    return {"x": bf(np.random.standard_normal((B, D_IN)) * s),
            "W1o": bf(np.random.standard_normal((D_IN, D_H)) / np.sqrt(D_IN) / s[:, None] * t),
            "b1o": bf(np.random.standard_normal(D_H) * 0.2 * t),
            "W2o": bf(np.random.standard_normal((D_H, C)) * G / np.sqrt(D_H) / t[:, None]),
            "b2o": bf(np.random.standard_normal(C) * GB),
            "W1f": bf(np.random.standard_normal((D_IN, D_H)) / np.sqrt(D_IN) / s[:, None] * t),
            "b1f": bf(np.random.standard_normal(D_H) * 0.2 * t),
            "W2f": bf(np.random.standard_normal((D_H, C)) * G / np.sqrt(D_H) / t[:, None]),
            "b2f": bf(np.random.standard_normal(C) * GB)}


def reference(x, W1o, b1o, W2o, b2o, W1f, b1f, W2f, b2f):
    xq = mxq(f64(x), 1, "e4m3")
    x1 = mlp(xq, W1o, b1o, W2o, b2o)
    x2 = mlp(xq, W1f, b1f, W2f, b2f)
    cond_in = comp_max_tau(x1, TAU, T1, T2)
    return x1 * (1.0 - cond_in[:, None]) + x2 * cond_in[:, None]

@@ -1,0 +1,381 @@
+from contextlib import ExitStack
+
+import concourse.mybir as mybir
+from concourse.masks import make_identity
+
+F32 = mybir.dt.float32
+BF16 = mybir.dt.bfloat16
+U32 = mybir.dt.uint32
+U8 = mybir.dt.uint8
+FP8X4 = mybir.dt.float8_e4m3fn_x4
+ACT = mybir.ActivationFunctionType
+ALU = mybir.AluOpType
+AXIS = mybir.AxisListType
+
+P = 128
+PACK = 4
+ROWS, D_IN, D_H, CLASSES = 8192, 512, 512, 128
+TILES = ROWS // P
+GROUP_TILES = 4
+GROUP_ROWS = GROUP_TILES * P
+GROUPS = TILES // GROUP_TILES
+STEPS = 2 * GROUPS
+HALF_GROUPS = GROUPS // 2
+HALF_TILES = TILES // 2
+WORDS = D_IN // 2
+TAU = 0.5
+SERIES_STEPS = 3
+
+FLOPS = 2 * (2 * ROWS * D_IN * D_H + 2 * ROWS * D_H * CLASSES)
+
+
+def quantise(nc, grouped, codes, scales):
+    nc.vector.quantize_mx(out=codes.bitcast(FP8X4), scales=scales, in_=grouped)
+
+
+def mx_pass(nc, acc, stationary, moving):
+    nc.tensor.matmul_mx(
+        out=acc,
+        lhsT=stationary[0].bitcast(FP8X4),
+        lhsT_scale=stationary[1],
+        rhs=moving[0].bitcast(FP8X4),
+        rhs_scale=moving[1],
+        start=True,
+        stop=True,
+    )
+
+
+def copy_on(engine, out, in_):
+    engine.tensor_scalar(out=out, in0=in_, scalar1=1.0, scalar2=0.0, op0=ALU.mult, op1=ALU.add)
+
+
+def stage_network(nc, keep, net, engine, w1, b1, w2, b2):
+    w1_raw = keep.tile([P, PACK, D_H], BF16, name="w1_raw_" + net)
+    nc.scalar.dma_start(out=w1_raw[:], in_=w1.rearrange("(p j) h -> p j h", j=PACK))
+    w1_grouped = keep.tile([P, D_H, PACK], BF16, name="w1_grouped_" + net, align_bytes=64)
+    copy_on(
+        engine,
+        w1_grouped[:].rearrange("p (t m) j -> p t m j", t=PACK),
+        w1_raw[:].rearrange("p j (m t) -> p t m j", t=PACK),
+    )
+    b1_raw = keep.tile([P, PACK], BF16, name="b1_raw_" + net)
+    nc.scalar.dma_start(out=b1_raw[:], in_=b1.rearrange("(p t) -> p t", t=PACK))
+    b1_cols = keep.tile([P, PACK], F32, name="b1_cols_" + net)
+    copy_on(engine, b1_cols[:], b1_raw[:])
+    w2_raw = keep.tile([P, PACK, CLASSES], BF16, name="w2_raw_" + net)
+    nc.scalar.dma_start(out=w2_raw[:], in_=w2.rearrange("(p t) c -> p t c", t=PACK))
+    w2_grouped = keep.tile([P, CLASSES, PACK], BF16, name="w2_grouped_" + net, align_bytes=64)
+    copy_on(engine, w2_grouped[:], w2_raw[:].rearrange("p t c -> p c t"))
+    b2_raw = keep.tile([P, CLASSES], BF16, name="b2_raw_" + net)
+    nc.scalar.dma_start(out=b2_raw[:], in_=b2.partition_broadcast(P))
+    b2_rows = keep.tile([P, CLASSES], F32, name="b2_rows_" + net)
+    copy_on(engine, b2_rows[:], b2_raw[:])
+    return {
+        "w1_grouped": w1_grouped,
+        "w2_grouped": w2_grouped,
+        "w1": (
+            keep.tile([P, D_H], U32, name="w1_codes_" + net, align_bytes=64),
+            keep.tile([P, D_H], U8, name="w1_scales_" + net, align_bytes=64),
+        ),
+        "w2": (
+            keep.tile([P, CLASSES], U32, name="w2_codes_" + net, align_bytes=64),
+            keep.tile([P, CLASSES], U8, name="w2_scales_" + net, align_bytes=64),
+        ),
+        "b1": b1_cols,
+        "b2": b2_rows,
+    }
+
+
+def quantise_network(nc, net):
+    quantise(nc, net["w1_grouped"][:].rearrange("p c j -> p (c j)"), net["w1"][0][:], net["w1"][1][:])
+    quantise(nc, net["w2_grouped"][:].rearrange("p c t -> p (c t)"), net["w2"][0][:], net["w2"][1][:])
+
+
+def gp_affine(nc, out, in_, mul, add):
+    nc.gpsimd.tensor_scalar(out=out, in0=in_, scalar1=mul, scalar2=add, op0=ALU.mult, op1=ALU.add)
+
+
+def gp_mul(nc, out, in0, in1):
+    nc.gpsimd.tensor_tensor(out=out, in0=in0, in1=in1, op=ALU.mult)
+
+
+def inverse_series(nc, gate, total, m, name):
+    b = gate.tile([P, HALF_TILES], F32, name="b_" + name)
+    a = gate.tile([P, HALF_TILES], F32, name="a_" + name)
+    one_plus_b = gate.tile([P, HALF_TILES], F32, name="one_plus_b_" + name)
+    gp_affine(nc, b[:], total, -2.0 / m, 1.0)
+    gp_affine(nc, a[:], b[:], 1.0, 1.0)
+    for step in range(SERIES_STEPS):
+        gp_mul(nc, b[:], b[:], b[:])
+        gp_affine(nc, one_plus_b[:], b[:], 1.0, 1.0)
+        gp_mul(nc, a[:], a[:], one_plus_b[:])
+    return a
+
+
+def gate_weights(nc, gate, sums, half):
+    cols = slice(half * HALF_TILES, (half + 1) * HALF_TILES)
+    tag = "_%d" % half
+
+    def new(name):
+        return gate.tile([P, HALF_TILES], F32, name=name + tag)
+
+    recip1, recip2, recip4, recip8 = new("recip1"), new("recip2"), new("recip4"), new("recip8")
+    nc.vector.reciprocal(out=recip1[:], in_=sums["e1"][:, cols])
+    gp_mul(nc, recip2[:], recip1[:], recip1[:])
+    gp_mul(nc, recip4[:], recip2[:], recip2[:])
+    gp_mul(nc, recip8[:], recip4[:], recip4[:])
+
+    total0, inv0, scale1 = new("total0"), new("inv0"), new("scale1")
+    gp_mul(nc, total0[:], sums["e2"][:, cols], recip2[:])
+    gp_affine(nc, total0[:], total0[:], 1.0, TAU**2)
+    m0 = 2.0 + TAU**2
+    a0 = inverse_series(nc, gate, total0[:], m0, "0" + tag)
+    gp_affine(nc, inv0[:], a0[:], 2.0 / m0, 0.0)
+    gp_mul(nc, scale1[:], inv0[:], inv0[:])
+
+    total1, scale2 = new("total1"), new("scale2")
+    gp_mul(nc, total1[:], sums["e4"][:, cols], recip4[:])
+    gp_affine(nc, total1[:], total1[:], 1.0, TAU**4)
+    gp_mul(nc, total1[:], total1[:], scale1[:])
+    a1 = inverse_series(nc, gate, total1[:], 2.0, "1" + tag)
+    gp_mul(nc, scale2[:], scale1[:], a1[:])
+    gp_mul(nc, scale2[:], scale2[:], scale2[:])
+
+    total2, cond, alpha = new("total2"), new("cond"), new("alpha")
+    gp_mul(nc, total2[:], sums["e8"][:, cols], recip8[:])
+    gp_affine(nc, total2[:], total2[:], 1.0, TAU**8)
+    gp_mul(nc, total2[:], total2[:], scale2[:])
+    a2 = inverse_series(nc, gate, total2[:], 2.0, "2" + tag)
+    gp_mul(nc, cond[:], scale2[:], a2[:])
+    gp_affine(nc, cond[:], cond[:], TAU**8, 0.0)
+
+    gp_affine(nc, alpha[:], cond[:], -1.0, 1.0)
+    gp_mul(nc, alpha[:], alpha[:], recip1[:])
+    return cond, alpha
+
+
+def tile_combnethe_pa_t_kernel(tc, x, W1o, b1o, W2o, b2o, W1f, b1f, W2f, b2f, out):
+    nc = tc.nc
+    x_rows = x.rearrange("(p j) k -> p j k", j=TILES)
+    out_rows = out.rearrange("(p j) c -> p j c", j=TILES)
+
+    with ExitStack() as pools:
+        pools.enter_context(tc.manual_schedule())
+        keep = pools.enter_context(tc.tile_pool(name="keep", bufs=1))
+        gate = pools.enter_context(tc.tile_pool(name="gate", bufs=1))
+        two = pools.enter_context(tc.tile_pool(name="two", bufs=2))
+        three = pools.enter_context(tc.tile_pool(name="three", bufs=3))
+        psum_x = pools.enter_context(tc.psum_pool(name="psum_x", bufs=2))
+        psum_z = pools.enter_context(tc.psum_pool(name="psum_z", bufs=4))
+        psum_l = pools.enter_context(tc.psum_pool(name="psum_l", bufs=2))
+
+        identity = keep.tile([P, P], F32, name="identity")
+        make_identity(nc, identity[:])
+        nets = [
+            stage_network(nc, keep, "o", nc.vector, W1o, b1o, W2o, b2o),
+            stage_network(nc, keep, "f", nc.gpsimd, W1f, b1f, W2f, b2f),
+        ]
+        quantise_network(nc, nets[0])
+
+        sums = {}
+        for power in ("e1", "e2", "e4", "e8"):
+            sums[power] = gate.tile([P, TILES], F32, name="sum_" + power)
+        cond, alpha = [], []
+        x_sb, x_t, x_grouped, x_q = {}, {}, {}, {}
+        planes, z_left, h_grouped, h_q, acc, logits, neg_max, e, e_sum, beta = {}, {}, {}, {}, {}, {}, {}, {}, {}, {}
+
+        def load_x(g):
+            x_sb[g] = three.tile([P, GROUP_TILES * D_IN], BF16, name="x_sb")
+            nc.sync.dma_start(
+                out=x_sb[g][:].rearrange("p (j k) -> p j k", j=GROUP_TILES),
+                in_=x_rows[:, g * GROUP_TILES : (g + 1) * GROUP_TILES, :],
+            )
+
+        def transpose_x(g):
+            x_words = x_sb[g][:].bitcast(F32)
+            x_t[g] = []
+            for half in range(2):
+                bank = psum_x.tile([P, 2, 2, P], F32, name="x_t")
+                for jj in range(2):
+                    for u in range(2):
+                        first = (2 * half + jj) * WORDS
+                        nc.tensor.transpose(bank[:, jj, u, :], x_words[:, first + u : first + WORDS : 2], identity[:])
+                x_t[g].append(bank)
+
+        def copy_x_out(g, half):
+            if half == 0:
+                x_grouped[g] = two.tile([P, GROUP_ROWS * PACK], BF16, name="x_grouped", align_bytes=64)
+            grouped_words = x_grouped[g][:].bitcast(F32)
+            nc.vector.tensor_copy(
+                out=grouped_words[:, half * 2 * WORDS : (half + 1) * 2 * WORDS].rearrange(
+                    "p (j r u) -> p j r u", j=2, u=2
+                ),
+                in_=x_t[g][half][:].rearrange("p j u r -> p j r u"),
+            )
+
+        def quantise_x(g):
+            x_q[g] = (
+                keep.tile([P, GROUP_ROWS], U32, name="x_codes_%d" % g, align_bytes=64),
+                keep.tile([P, GROUP_ROWS], U8, name="x_scales_%d" % g, align_bytes=64),
+            )
+            quantise(nc, x_grouped[g][:], x_q[g][0][:], x_q[g][1][:])
+
+        def hidden_layer(s):
+            net = nets[s // GROUPS]
+            codes, scales = net["w1"]
+            rows = x_q[s % GROUPS]
+            planes[s] = two.tile([P, PACK, GROUP_ROWS], BF16, name="planes")
+            for t in range(PACK):
+                z = psum_z.tile([P, GROUP_ROWS], F32, name="z")
+                cols = slice(t * P, (t + 1) * P)
+                mx_pass(nc, z[:], (codes[:, cols], scales[:, cols]), (rows[0][:], rows[1][:]))
+                if t == PACK - 1 and s < GROUPS and s % 2 == 1:
+                    z_left[s] = z
+                else:
+                    nc.scalar.activation(
+                        out=planes[s][:, t, :], in_=z[:], func=ACT.Relu, bias=net["b1"][:, t : t + 1], scale=1.0
+                    )
+
+        def vector_relu(s):
+            if s in z_left:
+                t = PACK - 1
+                nc.vector.tensor_scalar(
+                    out=planes[s][:, t, :],
+                    in0=z_left[s][:],
+                    scalar1=nets[s // GROUPS]["b1"][:, t : t + 1],
+                    scalar2=0.0,
+                    op0=ALU.add,
+                    op1=ALU.max,
+                )
+
+        def regroup_h(s):
+            h_grouped[s] = two.tile([P, GROUP_ROWS, PACK], BF16, name="h_grouped", align_bytes=64)
+            nc.vector.tensor_copy(
+                out=h_grouped[s][:].rearrange("p (c i) t -> p c t i", i=4),
+                in_=planes[s][:].rearrange("p t (c i) -> p c t i", i=4),
+            )
+
+        def quantise_h(s):
+            h_q[s] = (
+                two.tile([P, GROUP_ROWS], U32, name="h_codes", align_bytes=64),
+                two.tile([P, GROUP_ROWS], U8, name="h_scales", align_bytes=64),
+            )
+            quantise(nc, h_grouped[s][:].rearrange("p r t -> p (r t)"), h_q[s][0][:], h_q[s][1][:])
+
+        def head(s):
+            w2 = nets[s // GROUPS]["w2"]
+            acc[s] = psum_l.tile([P, GROUP_TILES, CLASSES], F32, name="acc")
+            for j in range(GROUP_TILES):
+                cols = slice(j * P, (j + 1) * P)
+                mx_pass(nc, acc[s][:, j, :], (h_q[s][0][:, cols], h_q[s][1][:, cols]), (w2[0][:], w2[1][:]))
+
+        def add_bias(s):
+            logits[s] = three.tile([P, GROUP_TILES, CLASSES], F32, name="logits")
+            nc.vector.tensor_tensor(
+                out=logits[s][:],
+                in0=acc[s][:],
+                in1=nets[s // GROUPS]["b2"][:].unsqueeze(1).to_broadcast([P, GROUP_TILES, CLASSES]),
+                op=ALU.add,
+            )
+
+        def row_max(s):
+            neg_max[s] = three.tile([P, GROUP_TILES], F32, name="neg_max")
+            nc.vector.tensor_reduce(out=neg_max[s][:], in_=logits[s][:], axis=AXIS.X, op=ALU.max, negate=True)
+
+        def exponentials(s):
+            if s < GROUPS:
+                e[s] = keep.tile([P, GROUP_TILES, CLASSES], F32, name="e_o_%d" % s)
+                e_sum[s] = sums["e1"][:, s * GROUP_TILES : (s + 1) * GROUP_TILES]
+            else:
+                e[s] = three.tile([P, GROUP_TILES, CLASSES], F32, name="e_f")
+                e_sum[s] = three.tile([P, GROUP_TILES], F32, name="sum_f")
+            for j in range(GROUP_TILES):
+                nc.scalar.activation(
+                    out=e[s][:, j, :],
+                    in_=logits[s][:, j, :],
+                    func=ACT.Exp,
+                    bias=neg_max[s][:, j : j + 1],
+                    scale=1.0,
+                    accum_out=e_sum[s][:, j : j + 1],
+                )
+
+        def power_sums(s):
+            powers = two.tile([P, GROUP_TILES, CLASSES], F32, name="powers")
+            for power in ("e2", "e4", "e8"):
+                for j in range(GROUP_TILES):
+                    nc.scalar.activation(
+                        out=powers[:, j, :],
+                        in_=e[s][:, j, :] if power == "e2" else powers[:, j, :],
+                        func=ACT.Square,
+                        accum_out=sums[power][:, s * GROUP_TILES + j : s * GROUP_TILES + j + 1],
+                    )
+
+        def gate_half(half):
+            cond_half, alpha_half = gate_weights(nc, gate, sums, half)
+            cond.append(cond_half)
+            alpha.append(alpha_half)
+
+        def blend_scale_o(s):
+            g = s - GROUPS
+            for j in range(GROUP_TILES):
+                column = (g % HALF_GROUPS) * GROUP_TILES + j
+                nc.scalar.activation(
+                    out=e[g][:, j, :],
+                    in_=e[g][:, j, :],
+                    func=ACT.Copy,
+                    scale=alpha[g // HALF_GROUPS][:, column : column + 1],
+                )
+
+        def blend_reciprocal(s):
+            beta[s] = three.tile([P, GROUP_TILES], F32, name="beta")
+            nc.vector.reciprocal(out=beta[s][:], in_=e_sum[s][:])
+
+        def blend_beta(s):
+            g = s - GROUPS
+            member = g % HALF_GROUPS
+            nc.vector.tensor_mul(
+                out=beta[s][:],
+                in0=beta[s][:],
+                in1=cond[g // HALF_GROUPS][:, member * GROUP_TILES : (member + 1) * GROUP_TILES],
+            )
+
+        def blend_and_store(s):
+            g = s - GROUPS
+            for j in range(GROUP_TILES):
+                nc.vector.scalar_tensor_tensor(
+                    out=e[s][:, j, :],
+                    in0=e[s][:, j, :],
+                    scalar=beta[s][:, j : j + 1],
+                    in1=e[g][:, j, :],
+                    op0=ALU.mult,
+                    op1=ALU.add,
+                )
+            nc.sync.dma_start(out=out_rows[:, g * GROUP_TILES : (g + 1) * GROUP_TILES, :], in_=e[s][:])
+
+        def run(stage, index, first, last):
+            if first <= index < last:
+                stage(index)
+
+        for i in range(-4, STEPS + 4):
+            run(load_x, i + 4, 0, GROUPS)
+            run(hidden_layer, i + 1, 0, STEPS)
+            run(regroup_h, i, 0, STEPS)
+            run(lambda g: copy_x_out(g, 0), i + 2, 0, GROUPS)
+            run(blend_reciprocal, i - 3, GROUPS, STEPS)
+            run(quantise_h, i, 0, STEPS)
+            run(lambda g: copy_x_out(g, 1), i + 2, 0, GROUPS)
+            run(vector_relu, i + 1, 0, GROUPS)
+            run(transpose_x, i + 3, 0, GROUPS)
+            run(head, i, 0, STEPS)
+            run(add_bias, i - 1, 0, STEPS)
+            run(quantise_x, i + 2, 0, GROUPS)
+            run(blend_beta, i - 3, GROUPS, STEPS)
+            run(row_max, i - 1, 0, STEPS)
+            run(exponentials, i - 2, 0, STEPS)
+            run(power_sums, i - 2, 0, GROUPS)
+            run(blend_scale_o, i - 2, GROUPS, STEPS)
+            run(blend_and_store, i - 3, GROUPS, STEPS)
+            if i == 0:
+                quantise_network(nc, nets[1])
+            if i - 3 in (HALF_GROUPS - 1, GROUPS - 1):
+                gate_half((i - 3) // HALF_GROUPS)

@@ -91,67 +91,67 @@ def quantise_network(nc, net):
     quantise(nc, net["w2_grouped"][:].rearrange("p c t -> p (c t)"), net["w2"][0][:], net["w2"][1][:])
 
 
-def gp_affine(nc, out, in_, mul, add):
-    nc.gpsimd.tensor_scalar(out=out, in0=in_, scalar1=mul, scalar2=add, op0=ALU.mult, op1=ALU.add)
-
-
-def gp_mul(nc, out, in0, in1):
-    nc.gpsimd.tensor_tensor(out=out, in0=in0, in1=in1, op=ALU.mult)
-
-
-def inverse_series(nc, gate, total, m, name):
-    b = gate.tile([P, HALF_TILES], F32, name="b_" + name)
-    a = gate.tile([P, HALF_TILES], F32, name="a_" + name)
-    one_plus_b = gate.tile([P, HALF_TILES], F32, name="one_plus_b_" + name)
-    gp_affine(nc, b[:], total, -2.0 / m, 1.0)
-    gp_affine(nc, a[:], b[:], 1.0, 1.0)
-    for step in range(SERIES_STEPS):
-        gp_mul(nc, b[:], b[:], b[:])
-        gp_affine(nc, one_plus_b[:], b[:], 1.0, 1.0)
-        gp_mul(nc, a[:], a[:], one_plus_b[:])
-    return a
-
-
-def gate_weights(nc, gate, sums, half):
+def gate_slots(nc, gate, sums, half):
     cols = slice(half * HALF_TILES, (half + 1) * HALF_TILES)
     tag = "_%d" % half
+    slots = []
 
     def new(name):
         return gate.tile([P, HALF_TILES], F32, name=name + tag)
 
+    def mul(out, in0, in1):
+        return lambda: nc.vector.tensor_tensor(out=out[:], in0=in0, in1=in1, op=ALU.mult)
+
+    def affine(out, in_, factor, shift):
+        return lambda: nc.vector.tensor_scalar(
+            out=out[:], in0=in_[:], scalar1=factor, scalar2=shift, op0=ALU.mult, op1=ALU.add
+        )
+
+    def fused(out, in0, scalar, op0, in1):
+        return lambda: nc.vector.scalar_tensor_tensor(
+            out=out[:], in0=in0[:], scalar=scalar, in1=in1[:], op0=op0, op1=ALU.mult
+        )
+
+    def series(total, factor, shift, name, fill):
+        b = [new("b0_" + name), new("b1_" + name)]
+        a = new("a_" + name)
+        slots.append([affine(b[0], total, factor, shift)] + fill[:1])
+        slots.append([affine(a, b[0], 1.0, 1.0), mul(b[1], b[0][:], b[0][:])])
+        slots.append([mul(b[0], b[1][:], b[1][:]), fused(a, b[1], 1.0, ALU.add, a)])
+        slots.append([mul(b[1], b[0][:], b[0][:]), fused(a, b[0], 1.0, ALU.add, a)])
+        slots.append([fused(a, b[1], 1.0, ALU.add, a)] + fill[1:2])
+        return a
+
+    c0 = 2.0 / (2.0 + TAU**2)
     recip1, recip2, recip4, recip8 = new("recip1"), new("recip2"), new("recip4"), new("recip8")
-    nc.vector.reciprocal(out=recip1[:], in_=sums["e1"][:, cols])
-    gp_mul(nc, recip2[:], recip1[:], recip1[:])
-    gp_mul(nc, recip4[:], recip2[:], recip2[:])
-    gp_mul(nc, recip8[:], recip4[:], recip4[:])
+    part0, part1, part2 = new("part0"), new("part1"), new("part2")
+    slots.append([lambda: nc.vector.reciprocal(out=recip1[:], in_=sums["e1"][:, cols])])
+    slots.append([mul(recip2, recip1[:], recip1[:])])
+    slots.append([mul(part0, sums["e2"][:, cols], recip2[:]), mul(recip4, recip2[:], recip2[:])])
 
-    total0, inv0, scale1 = new("total0"), new("inv0"), new("scale1")
-    gp_mul(nc, total0[:], sums["e2"][:, cols], recip2[:])
-    gp_affine(nc, total0[:], total0[:], 1.0, TAU**2)
-    m0 = 2.0 + TAU**2
-    a0 = inverse_series(nc, gate, total0[:], m0, "0" + tag)
-    gp_affine(nc, inv0[:], a0[:], 2.0 / m0, 0.0)
-    gp_mul(nc, scale1[:], inv0[:], inv0[:])
+    a0 = series(
+        part0,
+        -c0,
+        1.0 - c0 * TAU**2,
+        "0",
+        [mul(part1, sums["e4"][:, cols], recip4[:]), mul(recip8, recip4[:], recip4[:])],
+    )
 
-    total1, scale2 = new("total1"), new("scale2")
-    gp_mul(nc, total1[:], sums["e4"][:, cols], recip4[:])
-    gp_affine(nc, total1[:], total1[:], 1.0, TAU**4)
-    gp_mul(nc, total1[:], total1[:], scale1[:])
-    a1 = inverse_series(nc, gate, total1[:], 2.0, "1" + tag)
-    gp_mul(nc, scale2[:], scale1[:], a1[:])
-    gp_mul(nc, scale2[:], scale2[:], scale2[:])
+    square0, rest1 = new("square0"), new("rest1")
+    slots.append([mul(square0, a0[:], a0[:]), mul(part2, sums["e8"][:, cols], recip8[:])])
+    slots.append([fused(rest1, part1, TAU**4, ALU.add, square0)])
+    a1 = series(rest1, -(c0**2), 1.0, "1", [])
 
-    total2, cond, alpha = new("total2"), new("cond"), new("alpha")
-    gp_mul(nc, total2[:], sums["e8"][:, cols], recip8[:])
-    gp_affine(nc, total2[:], total2[:], 1.0, TAU**8)
-    gp_mul(nc, total2[:], total2[:], scale2[:])
-    a2 = inverse_series(nc, gate, total2[:], 2.0, "2" + tag)
-    gp_mul(nc, cond[:], scale2[:], a2[:])
-    gp_affine(nc, cond[:], cond[:], TAU**8, 0.0)
+    both, square1, rest2 = new("both"), new("square1"), new("rest2")
+    slots.append([mul(both, square0[:], a1[:])])
+    slots.append([mul(square1, both[:], both[:])])
+    slots.append([fused(rest2, part2, TAU**8, ALU.add, square1)])
+    a2 = series(rest2, -(c0**4), 1.0, "2", [])
 
-    gp_affine(nc, alpha[:], cond[:], -1.0, 1.0)
-    gp_mul(nc, alpha[:], alpha[:], recip1[:])
-    return cond, alpha
+    minus_cond, alpha = new("minus_cond"), new("alpha")
+    slots.append([fused(minus_cond, square1, -(TAU**8) * c0**4, ALU.mult, a2)])
+    slots.append([fused(alpha, minus_cond, 1.0, ALU.add, recip1)])
+    return slots, minus_cond, alpha
 
 
 def tile_combnethe_pa_t_kernel(tc, x, W1o, b1o, W2o, b2o, W1f, b1f, W2f, b2f, out):
@@ -180,7 +180,8 @@ def tile_combnethe_pa_t_kernel(tc, x, W1o, b1o, W2o, b2o, W1f, b1f, W2f, b2f, ou
         sums = {}
         for power in ("e1", "e2", "e4", "e8"):
             sums[power] = gate.tile([P, TILES], F32, name="sum_" + power)
-        cond, alpha = [], []
+        minus_cond, alpha = [], []
+        waiting, issued = [], [0]
         x_sb, x_t, x_grouped, x_q = {}, {}, {}, {}
         planes, z_left, h_grouped, h_q, acc, logits, neg_max, e, e_sum, beta = {}, {}, {}, {}, {}, {}, {}, {}, {}, {}
 
@@ -311,12 +312,20 @@ def tile_combnethe_pa_t_kernel(tc, x, W1o, b1o, W2o, b2o, W1f, b1f, W2f, b2f, ou
                     )
 
         def gate_half(half):
-            cond_half, alpha_half = gate_weights(nc, gate, sums, half)
-            cond.append(cond_half)
+            slots, minus_cond_half, alpha_half = gate_slots(nc, gate, sums, half)
+            waiting.extend(slots)
+            minus_cond.append(minus_cond_half)
             alpha.append(alpha_half)
+
+        def gate_slot():
+            if issued[0] < len(waiting):
+                for instruction in waiting[issued[0]]:
+                    instruction()
+                issued[0] += 1
 
         def blend_scale_o(s):
             g = s - GROUPS
+            assert issued[0] == len(waiting) or g % HALF_GROUPS > 0
             for j in range(GROUP_TILES):
                 column = (g % HALF_GROUPS) * GROUP_TILES + j
                 nc.scalar.activation(
@@ -333,10 +342,13 @@ def tile_combnethe_pa_t_kernel(tc, x, W1o, b1o, W2o, b2o, W1f, b1f, W2f, b2f, ou
         def blend_beta(s):
             g = s - GROUPS
             member = g % HALF_GROUPS
-            nc.vector.tensor_mul(
+            nc.vector.scalar_tensor_tensor(
                 out=beta[s][:],
                 in0=beta[s][:],
-                in1=cond[g // HALF_GROUPS][:, member * GROUP_TILES : (member + 1) * GROUP_TILES],
+                scalar=-1.0,
+                in1=minus_cond[g // HALF_GROUPS][:, member * GROUP_TILES : (member + 1) * GROUP_TILES],
+                op0=ALU.mult,
+                op1=ALU.mult,
             )
 
         def blend_and_store(s):
@@ -360,17 +372,21 @@ def tile_combnethe_pa_t_kernel(tc, x, W1o, b1o, W2o, b2o, W1f, b1f, W2f, b2f, ou
             run(load_x, i + 4, 0, GROUPS)
             run(hidden_layer, i + 1, 0, STEPS)
             run(regroup_h, i, 0, STEPS)
+            gate_slot()
             run(lambda g: copy_x_out(g, 0), i + 2, 0, GROUPS)
             run(blend_reciprocal, i - 3, GROUPS, STEPS)
             run(quantise_h, i, 0, STEPS)
+            gate_slot()
             run(lambda g: copy_x_out(g, 1), i + 2, 0, GROUPS)
             run(vector_relu, i + 1, 0, GROUPS)
             run(transpose_x, i + 3, 0, GROUPS)
             run(head, i, 0, STEPS)
             run(add_bias, i - 1, 0, STEPS)
+            gate_slot()
             run(quantise_x, i + 2, 0, GROUPS)
             run(blend_beta, i - 3, GROUPS, STEPS)
             run(row_max, i - 1, 0, STEPS)
+            gate_slot()
             run(exponentials, i - 2, 0, STEPS)
             run(power_sums, i - 2, 0, GROUPS)
             run(blend_scale_o, i - 2, GROUPS, STEPS)
@@ -378,4 +394,5 @@ def tile_combnethe_pa_t_kernel(tc, x, W1o, b1o, W2o, b2o, W1f, b1f, W2f, b2f, ou
             if i == 0:
                 quantise_network(nc, nets[1])
             if i - 3 in (HALF_GROUPS - 1, GROUPS - 1):
+                assert issued[0] == len(waiting)
                 gate_half((i - 3) // HALF_GROUPS)

@@ -373,19 +373,28 @@ def tile_combnethe_pa_t_kernel(tc, x, W1o, b1o, W2o, b2o, W1f, b1f, W2f, b2f, ou
             run(hidden_layer, i + 1, 0, STEPS)
             run(regroup_h, i, 0, STEPS)
             gate_slot()
-            run(lambda g: copy_x_out(g, 0), i + 2, 0, GROUPS)
-            run(blend_reciprocal, i - 3, GROUPS, STEPS)
-            run(quantise_h, i, 0, STEPS)
-            gate_slot()
-            run(lambda g: copy_x_out(g, 1), i + 2, 0, GROUPS)
-            run(vector_relu, i + 1, 0, GROUPS)
-            run(transpose_x, i + 3, 0, GROUPS)
-            run(head, i, 0, STEPS)
-            run(add_bias, i - 1, 0, STEPS)
-            gate_slot()
-            run(quantise_x, i + 2, 0, GROUPS)
-            run(blend_beta, i - 3, GROUPS, STEPS)
-            run(row_max, i - 1, 0, STEPS)
+            if i + 2 < GROUPS:
+                run(lambda g: copy_x_out(g, 0), i + 2, 0, GROUPS)
+                run(quantise_h, i, 0, STEPS)
+                gate_slot()
+                run(lambda g: copy_x_out(g, 1), i + 2, 0, GROUPS)
+                run(vector_relu, i + 1, 0, GROUPS)
+                run(transpose_x, i + 3, 0, GROUPS)
+                run(head, i, 0, STEPS)
+                run(add_bias, i - 1, 0, STEPS)
+                gate_slot()
+                run(quantise_x, i + 2, 0, GROUPS)
+                run(row_max, i - 1, 0, STEPS)
+            else:
+                run(blend_reciprocal, i - 3, GROUPS, STEPS)
+                run(add_bias, i - 1, 0, STEPS)
+                gate_slot()
+                run(quantise_h, i, 0, STEPS)
+                gate_slot()
+                run(vector_relu, i + 1, 0, GROUPS)
+                run(head, i, 0, STEPS)
+                run(blend_beta, i - 3, GROUPS, STEPS)
+                run(row_max, i - 1, 0, STEPS)
             gate_slot()
             run(exponentials, i - 2, 0, STEPS)
             run(power_sums, i - 2, 0, GROUPS)

@@ -183,7 +183,7 @@ def tile_combnethe_pa_t_kernel(tc, x, W1o, b1o, W2o, b2o, W1f, b1f, W2f, b2f, ou
         minus_cond, alpha = [], []
         waiting, issued = [], [0]
         x_sb, x_t, x_grouped, x_q = {}, {}, {}, {}
-        planes, z_left, h_grouped, h_q, acc, logits, neg_max, e, e_sum, beta = {}, {}, {}, {}, {}, {}, {}, {}, {}, {}
+        planes, z, h_grouped, h_q, acc, logits, neg_max, e, e_sum, beta = {}, {}, {}, {}, {}, {}, {}, {}, {}, {}
 
         def load_x(g):
             x_sb[g] = three.tile([P, GROUP_TILES * D_IN], BF16, name="x_sb")
@@ -221,33 +221,47 @@ def tile_combnethe_pa_t_kernel(tc, x, W1o, b1o, W2o, b2o, W1f, b1f, W2f, b2f, ou
             )
             quantise(nc, x_grouped[g][:], x_q[g][0][:], x_q[g][1][:])
 
-        def hidden_layer(s):
-            net = nets[s // GROUPS]
-            codes, scales = net["w1"]
-            rows = x_q[s % GROUPS]
-            planes[s] = two.tile([P, PACK, GROUP_ROWS], BF16, name="planes")
-            for t in range(PACK):
-                z = psum_z.tile([P, GROUP_ROWS], F32, name="z")
+        def vector_takes(s):
+            return 0 <= s < GROUPS and s % 2 == 1 or GROUPS - 1 <= s < GROUPS + 3
+
+        def hidden_product(s, t):
+            if s < STEPS:
+                codes, scales = nets[s // GROUPS]["w1"]
+                rows = x_q[s % GROUPS]
+                z[(s, t)] = psum_z.tile([P, GROUP_ROWS], F32, name="z")
                 cols = slice(t * P, (t + 1) * P)
-                mx_pass(nc, z[:], (codes[:, cols], scales[:, cols]), (rows[0][:], rows[1][:]))
-                if t == PACK - 1 and s < GROUPS and s % 2 == 1:
-                    z_left[s] = z
-                else:
-                    nc.scalar.activation(
-                        out=planes[s][:, t, :], in_=z[:], func=ACT.Relu, bias=net["b1"][:, t : t + 1], scale=1.0
-                    )
+                mx_pass(nc, z[(s, t)][:], (codes[:, cols], scales[:, cols]), (rows[0][:], rows[1][:]))
+
+        def hidden_layer(s):
+            if s >= 0:
+                planes[s] = two.tile([P, PACK, GROUP_ROWS], BF16, name="planes")
+            for t in range(PACK):
+                if t < PACK - 1 or not vector_takes(s):
+                    if s >= 0:
+                        nc.scalar.activation(
+                            out=planes[s][:, t, :],
+                            in_=z[(s, t)][:],
+                            func=ACT.Relu,
+                            bias=nets[s // GROUPS]["b1"][:, t : t + 1],
+                            scale=1.0,
+                        )
+                    hidden_product(s + 1, t)
 
         def vector_relu(s):
-            if s in z_left:
+            if vector_takes(s):
                 t = PACK - 1
                 nc.vector.tensor_scalar(
                     out=planes[s][:, t, :],
-                    in0=z_left[s][:],
+                    in0=z[(s, t)][:],
                     scalar1=nets[s // GROUPS]["b1"][:, t : t + 1],
                     scalar2=0.0,
                     op0=ALU.add,
                     op1=ALU.max,
                 )
+
+        def last_product(s):
+            if vector_takes(s):
+                hidden_product(s + 1, PACK - 1)
 
         def regroup_h(s):
             h_grouped[s] = two.tile([P, GROUP_ROWS, PACK], BF16, name="h_grouped", align_bytes=64)
@@ -368,22 +382,23 @@ def tile_combnethe_pa_t_kernel(tc, x, W1o, b1o, W2o, b2o, W1f, b1f, W2f, b2f, ou
             if first <= index < last:
                 stage(index)
 
-        for i in range(-4, STEPS + 4):
-            run(load_x, i + 4, 0, GROUPS)
-            run(hidden_layer, i + 1, 0, STEPS)
+        for i in range(-5, STEPS + 4):
+            run(load_x, i + 5, 0, GROUPS)
+            run(hidden_layer, i + 1, -1, STEPS)
             run(regroup_h, i, 0, STEPS)
             gate_slot()
-            if i + 2 < GROUPS:
-                run(lambda g: copy_x_out(g, 0), i + 2, 0, GROUPS)
+            if i + 3 < GROUPS:
+                run(lambda g: copy_x_out(g, 0), i + 3, 0, GROUPS)
                 run(quantise_h, i, 0, STEPS)
                 gate_slot()
-                run(lambda g: copy_x_out(g, 1), i + 2, 0, GROUPS)
-                run(vector_relu, i + 1, 0, GROUPS)
-                run(transpose_x, i + 3, 0, GROUPS)
+                run(lambda g: copy_x_out(g, 1), i + 3, 0, GROUPS)
+                run(vector_relu, i + 1, 0, STEPS)
+                run(transpose_x, i + 4, 0, GROUPS)
                 run(head, i, 0, STEPS)
+                run(last_product, i + 1, 0, STEPS)
                 run(add_bias, i - 1, 0, STEPS)
                 gate_slot()
-                run(quantise_x, i + 2, 0, GROUPS)
+                run(quantise_x, i + 3, 0, GROUPS)
                 run(row_max, i - 1, 0, STEPS)
             else:
                 run(blend_reciprocal, i - 3, GROUPS, STEPS)
@@ -391,8 +406,9 @@ def tile_combnethe_pa_t_kernel(tc, x, W1o, b1o, W2o, b2o, W1f, b1f, W2f, b2f, ou
                 gate_slot()
                 run(quantise_h, i, 0, STEPS)
                 gate_slot()
-                run(vector_relu, i + 1, 0, GROUPS)
+                run(vector_relu, i + 1, 0, STEPS)
                 run(head, i, 0, STEPS)
+                run(last_product, i + 1, 0, STEPS)
                 run(blend_beta, i - 3, GROUPS, STEPS)
                 run(row_max, i - 1, 0, STEPS)
             gate_slot()

@@ -45,34 +45,29 @@ def mx_pass(nc, acc, stationary, moving):
     )
 
 
-def copy_on(engine, out, in_):
-    engine.tensor_scalar(out=out, in0=in_, scalar1=1.0, scalar2=0.0, op0=ALU.mult, op1=ALU.add)
+def copy_on(nc, engine, out, in_):
+    if engine == "vector":
+        nc.vector.tensor_scalar(out=out, in0=in_, scalar1=1.0, scalar2=0.0, op0=ALU.mult, op1=ALU.add)
+    else:
+        nc.scalar.copy(out=out, in_=in_)
 
 
-def stage_network(nc, keep, net, engine, w1, b1, w2, b2):
+def load_network(nc, keep, net, w1, b1, w2, b2):
     w1_raw = keep.tile([P, PACK, D_H], BF16, name="w1_raw_" + net)
     nc.scalar.dma_start(out=w1_raw[:], in_=w1.rearrange("(p j) h -> p j h", j=PACK))
-    w1_grouped = keep.tile([P, D_H, PACK], BF16, name="w1_grouped_" + net, align_bytes=64)
-    copy_on(
-        engine,
-        w1_grouped[:].rearrange("p (t m) j -> p t m j", t=PACK),
-        w1_raw[:].rearrange("p j (m t) -> p t m j", t=PACK),
-    )
     b1_raw = keep.tile([P, PACK], BF16, name="b1_raw_" + net)
     nc.scalar.dma_start(out=b1_raw[:], in_=b1.rearrange("(p t) -> p t", t=PACK))
-    b1_cols = keep.tile([P, PACK], F32, name="b1_cols_" + net)
-    copy_on(engine, b1_cols[:], b1_raw[:])
     w2_raw = keep.tile([P, PACK, CLASSES], BF16, name="w2_raw_" + net)
     nc.scalar.dma_start(out=w2_raw[:], in_=w2.rearrange("(p t) c -> p t c", t=PACK))
-    w2_grouped = keep.tile([P, CLASSES, PACK], BF16, name="w2_grouped_" + net, align_bytes=64)
-    copy_on(engine, w2_grouped[:], w2_raw[:].rearrange("p t c -> p c t"))
     b2_raw = keep.tile([P, CLASSES], BF16, name="b2_raw_" + net)
     nc.scalar.dma_start(out=b2_raw[:], in_=b2.partition_broadcast(P))
-    b2_rows = keep.tile([P, CLASSES], F32, name="b2_rows_" + net)
-    copy_on(engine, b2_rows[:], b2_raw[:])
     return {
-        "w1_grouped": w1_grouped,
-        "w2_grouped": w2_grouped,
+        "w1_raw": w1_raw,
+        "b1_raw": b1_raw,
+        "w2_raw": w2_raw,
+        "b2_raw": b2_raw,
+        "w1_grouped": keep.tile([P, D_H, PACK], BF16, name="w1_grouped_" + net, align_bytes=64),
+        "w2_grouped": keep.tile([P, CLASSES, PACK], BF16, name="w2_grouped_" + net, align_bytes=64),
         "w1": (
             keep.tile([P, D_H], U32, name="w1_codes_" + net, align_bytes=64),
             keep.tile([P, D_H], U8, name="w1_scales_" + net, align_bytes=64),
@@ -81,9 +76,24 @@ def stage_network(nc, keep, net, engine, w1, b1, w2, b2):
             keep.tile([P, CLASSES], U32, name="w2_codes_" + net, align_bytes=64),
             keep.tile([P, CLASSES], U8, name="w2_scales_" + net, align_bytes=64),
         ),
-        "b1": b1_cols,
-        "b2": b2_rows,
+        "b1": keep.tile([P, PACK], F32, name="b1_cols_" + net),
+        "b2": keep.tile([P, CLASSES], F32, name="b2_rows_" + net),
     }
+
+
+def lay_out_w1(nc, engine, net, first, last):
+    copy_on(
+        nc,
+        engine,
+        net["w1_grouped"][:].rearrange("p (t m) j -> p t m j", t=PACK)[:, first:last],
+        net["w1_raw"][:].rearrange("p j (m t) -> p t m j", t=PACK)[:, first:last],
+    )
+
+
+def lay_out_rest(nc, engine, net):
+    copy_on(nc, engine, net["b1"][:], net["b1_raw"][:])
+    copy_on(nc, engine, net["w2_grouped"][:], net["w2_raw"][:].rearrange("p t c -> p c t"))
+    copy_on(nc, engine, net["b2"][:], net["b2_raw"][:])
 
 
 def quantise_network(nc, net):
@@ -171,10 +181,9 @@ def tile_combnethe_pa_t_kernel(tc, x, W1o, b1o, W2o, b2o, W1f, b1f, W2f, b2f, ou
 
         identity = keep.tile([P, P], F32, name="identity")
         make_identity(nc, identity[:])
-        nets = [
-            stage_network(nc, keep, "o", nc.vector, W1o, b1o, W2o, b2o),
-            stage_network(nc, keep, "f", nc.gpsimd, W1f, b1f, W2f, b2f),
-        ]
+        nets = [load_network(nc, keep, "o", W1o, b1o, W2o, b2o), load_network(nc, keep, "f", W1f, b1f, W2f, b2f)]
+        lay_out_w1(nc, "vector", nets[0], 0, PACK)
+        lay_out_rest(nc, "vector", nets[0])
         quantise_network(nc, nets[0])
 
         sums = {}
@@ -416,7 +425,11 @@ def tile_combnethe_pa_t_kernel(tc, x, W1o, b1o, W2o, b2o, W1f, b1f, W2f, b2f, ou
             run(power_sums, i - 2, 0, GROUPS)
             run(blend_scale_o, i - 2, GROUPS, STEPS)
             run(blend_and_store, i - 3, GROUPS, STEPS)
-            if i == 0:
+            if i == -1 or i == 0:
+                lay_out_w1(nc, "scalar", nets[1], 2 * (i + 1), 2 * (i + 2))
+            if i == 1:
+                lay_out_rest(nc, "scalar", nets[1])
+            if i == 3:
                 quantise_network(nc, nets[1])
             if i - 3 in (HALF_GROUPS - 1, GROUPS - 1):
                 assert issued[0] == len(waiting)

@@ -25,6 +25,7 @@ HALF_TILES = TILES // 2
 WORDS = D_IN // 2
 TAU = 0.5
 SERIES_STEPS = 3
+SCALAR_X_GROUPS = 2
 
 FLOPS = 2 * (2 * ROWS * D_IN * D_H + 2 * ROWS * D_H * CLASSES)
 
@@ -54,13 +55,13 @@ def copy_on(nc, engine, out, in_):
 
 def load_network(nc, keep, net, w1, b1, w2, b2):
     w1_raw = keep.tile([P, PACK, D_H], BF16, name="w1_raw_" + net)
-    nc.scalar.dma_start(out=w1_raw[:], in_=w1.rearrange("(p j) h -> p j h", j=PACK))
+    nc.sync.dma_start(out=w1_raw[:], in_=w1.rearrange("(p j) h -> p j h", j=PACK))
     b1_raw = keep.tile([P, PACK], BF16, name="b1_raw_" + net)
-    nc.scalar.dma_start(out=b1_raw[:], in_=b1.rearrange("(p t) -> p t", t=PACK))
+    nc.sync.dma_start(out=b1_raw[:], in_=b1.rearrange("(p t) -> p t", t=PACK))
     w2_raw = keep.tile([P, PACK, CLASSES], BF16, name="w2_raw_" + net)
-    nc.scalar.dma_start(out=w2_raw[:], in_=w2.rearrange("(p t) c -> p t c", t=PACK))
+    nc.sync.dma_start(out=w2_raw[:], in_=w2.rearrange("(p t) c -> p t c", t=PACK))
     b2_raw = keep.tile([P, CLASSES], BF16, name="b2_raw_" + net)
-    nc.scalar.dma_start(out=b2_raw[:], in_=b2.partition_broadcast(P))
+    nc.sync.dma_start(out=b2_raw[:], in_=b2.partition_broadcast(P))
     return {
         "w1_raw": w1_raw,
         "b1_raw": b1_raw,
@@ -175,17 +176,18 @@ def tile_combnethe_pa_t_kernel(tc, x, W1o, b1o, W2o, b2o, W1f, b1f, W2f, b2f, ou
         gate = pools.enter_context(tc.tile_pool(name="gate", bufs=1))
         two = pools.enter_context(tc.tile_pool(name="two", bufs=2))
         three = pools.enter_context(tc.tile_pool(name="three", bufs=3))
+        five = pools.enter_context(tc.tile_pool(name="five", bufs=5))
         psum_x = pools.enter_context(tc.psum_pool(name="psum_x", bufs=2))
         psum_z = pools.enter_context(tc.psum_pool(name="psum_z", bufs=4))
         psum_l = pools.enter_context(tc.psum_pool(name="psum_l", bufs=2))
 
         identity = keep.tile([P, P], F32, name="identity")
         make_identity(nc, identity[:])
-        nets = [load_network(nc, keep, "o", W1o, b1o, W2o, b2o), load_network(nc, keep, "f", W1f, b1f, W2f, b2f)]
-        lay_out_w1(nc, "vector", nets[0], 0, PACK)
-        lay_out_rest(nc, "vector", nets[0])
-        quantise_network(nc, nets[0])
+        warm = keep.tile([P, 1], F32, name="warm")
+        nc.gpsimd.memset(warm[:], 0.0)
+        nc.scalar.activation(out=warm[:], in_=warm[:], func=ACT.Exp)
 
+        nets = []
         sums = {}
         for power in ("e1", "e2", "e4", "e8"):
             sums[power] = gate.tile([P, TILES], F32, name="sum_" + power)
@@ -216,12 +218,12 @@ def tile_combnethe_pa_t_kernel(tc, x, W1o, b1o, W2o, b2o, W1f, b1f, W2f, b2f, ou
             if half == 0:
                 x_grouped[g] = two.tile([P, GROUP_ROWS * PACK], BF16, name="x_grouped", align_bytes=64)
             grouped_words = x_grouped[g][:].bitcast(F32)
-            nc.vector.tensor_copy(
-                out=grouped_words[:, half * 2 * WORDS : (half + 1) * 2 * WORDS].rearrange(
-                    "p (j r u) -> p j r u", j=2, u=2
-                ),
-                in_=x_t[g][half][:].rearrange("p j u r -> p j r u"),
-            )
+            out = grouped_words[:, half * 2 * WORDS : (half + 1) * 2 * WORDS].rearrange("p (j r u) -> p j r u", j=2, u=2)
+            in_ = x_t[g][half][:].rearrange("p j u r -> p j r u")
+            if g < SCALAR_X_GROUPS:
+                nc.scalar.copy(out=out, in_=in_)
+            else:
+                nc.vector.tensor_copy(out=out, in_=in_)
 
         def quantise_x(g):
             x_q[g] = (
@@ -230,8 +232,12 @@ def tile_combnethe_pa_t_kernel(tc, x, W1o, b1o, W2o, b2o, W1f, b1f, W2f, b2f, ou
             )
             quantise(nc, x_grouped[g][:], x_q[g][0][:], x_q[g][1][:])
 
-        def vector_takes(s):
-            return 0 <= s < GROUPS and s % 2 == 1 or GROUPS - 1 <= s < GROUPS + 3
+        def vector_banks(s):
+            if GROUPS - 2 <= s < GROUPS + 3:
+                return 2
+            if 0 <= s < GROUPS and s % 2 == 1:
+                return 1
+            return 0
 
         def hidden_product(s, t):
             if s < STEPS:
@@ -245,7 +251,7 @@ def tile_combnethe_pa_t_kernel(tc, x, W1o, b1o, W2o, b2o, W1f, b1f, W2f, b2f, ou
             if s >= 0:
                 planes[s] = two.tile([P, PACK, GROUP_ROWS], BF16, name="planes")
             for t in range(PACK):
-                if t < PACK - 1 or not vector_takes(s):
+                if t < PACK - vector_banks(s):
                     if s >= 0:
                         nc.scalar.activation(
                             out=planes[s][:, t, :],
@@ -257,8 +263,7 @@ def tile_combnethe_pa_t_kernel(tc, x, W1o, b1o, W2o, b2o, W1f, b1f, W2f, b2f, ou
                     hidden_product(s + 1, t)
 
         def vector_relu(s):
-            if vector_takes(s):
-                t = PACK - 1
+            for t in range(PACK - vector_banks(s), PACK):
                 nc.vector.tensor_scalar(
                     out=planes[s][:, t, :],
                     in0=z[(s, t)][:],
@@ -269,8 +274,8 @@ def tile_combnethe_pa_t_kernel(tc, x, W1o, b1o, W2o, b2o, W1f, b1f, W2f, b2f, ou
                 )
 
         def last_product(s):
-            if vector_takes(s):
-                hidden_product(s + 1, PACK - 1)
+            for t in range(PACK - vector_banks(s), PACK):
+                hidden_product(s + 1, t)
 
         def regroup_h(s):
             h_grouped[s] = two.tile([P, GROUP_ROWS, PACK], BF16, name="h_grouped", align_bytes=64)
@@ -311,7 +316,7 @@ def tile_combnethe_pa_t_kernel(tc, x, W1o, b1o, W2o, b2o, W1f, b1f, W2f, b2f, ou
                 e[s] = keep.tile([P, GROUP_TILES, CLASSES], F32, name="e_o_%d" % s)
                 e_sum[s] = sums["e1"][:, s * GROUP_TILES : (s + 1) * GROUP_TILES]
             else:
-                e[s] = three.tile([P, GROUP_TILES, CLASSES], F32, name="e_f")
+                e[s] = five.tile([P, GROUP_TILES, CLASSES], F32, name="e_f")
                 e_sum[s] = three.tile([P, GROUP_TILES], F32, name="sum_f")
             for j in range(GROUP_TILES):
                 nc.scalar.activation(
@@ -391,16 +396,28 @@ def tile_combnethe_pa_t_kernel(tc, x, W1o, b1o, W2o, b2o, W1f, b1f, W2f, b2f, ou
             if first <= index < last:
                 stage(index)
 
+        load_x(0)
+        nets.append(load_network(nc, keep, "o", W1o, b1o, W2o, b2o))
+        load_x(1)
+        load_x(2)
+        nets.append(load_network(nc, keep, "f", W1f, b1f, W2f, b2f))
+        lay_out_w1(nc, "vector", nets[0], 0, PACK)
+
         for i in range(-5, STEPS + 4):
-            run(load_x, i + 5, 0, GROUPS)
+            run(load_x, i + 5, 3, GROUPS)
+            if i + 3 < SCALAR_X_GROUPS:
+                run(lambda g: copy_x_out(g, 0), i + 3, 0, GROUPS)
+                run(lambda g: copy_x_out(g, 1), i + 3, 0, GROUPS)
+            if i == -3:
+                lay_out_rest(nc, "scalar", nets[0])
             run(hidden_layer, i + 1, -1, STEPS)
             run(regroup_h, i, 0, STEPS)
             gate_slot()
             if i + 3 < GROUPS:
-                run(lambda g: copy_x_out(g, 0), i + 3, 0, GROUPS)
+                run(lambda g: copy_x_out(g, 0), i + 3, SCALAR_X_GROUPS, GROUPS)
                 run(quantise_h, i, 0, STEPS)
                 gate_slot()
-                run(lambda g: copy_x_out(g, 1), i + 3, 0, GROUPS)
+                run(lambda g: copy_x_out(g, 1), i + 3, SCALAR_X_GROUPS, GROUPS)
                 run(vector_relu, i + 1, 0, STEPS)
                 run(transpose_x, i + 4, 0, GROUPS)
                 run(head, i, 0, STEPS)
@@ -425,6 +442,8 @@ def tile_combnethe_pa_t_kernel(tc, x, W1o, b1o, W2o, b2o, W1f, b1f, W2f, b2f, ou
             run(power_sums, i - 2, 0, GROUPS)
             run(blend_scale_o, i - 2, GROUPS, STEPS)
             run(blend_and_store, i - 3, GROUPS, STEPS)
+            if i == -3:
+                quantise_network(nc, nets[0])
             if i == -1 or i == 0:
                 lay_out_w1(nc, "scalar", nets[1], 2 * (i + 1), 2 * (i + 2))
             if i == 1:

@@ -235,7 +235,7 @@ def tile_combnethe_pa_t_kernel(tc, x, W1o, b1o, W2o, b2o, W1f, b1f, W2f, b2f, ou
         def vector_banks(s):
             if GROUPS - 2 <= s < GROUPS + 3:
                 return 2
-            if 0 <= s < GROUPS and s % 2 == 1:
+            if 0 <= s < GROUPS and (s % 4 == 3 or s == GROUPS - 3):
                 return 1
             return 0
 

@@ -61,7 +61,6 @@ def load_network(nc, keep, net, w1, b1, w2, b2):
     w2_raw = keep.tile([P, PACK, CLASSES], BF16, name="w2_raw_" + net)
     nc.sync.dma_start(out=w2_raw[:], in_=w2.rearrange("(p t) c -> p t c", t=PACK))
     b2_raw = keep.tile([P, CLASSES], BF16, name="b2_raw_" + net)
-    nc.sync.dma_start(out=b2_raw[:], in_=b2.partition_broadcast(P))
     return {
         "w1_raw": w1_raw,
         "b1_raw": b1_raw,
@@ -91,10 +90,13 @@ def lay_out_w1(nc, engine, net, first, last):
     )
 
 
+def load_b2(nc, net, b2):
+    nc.sync.dma_start(out=net["b2_raw"][:], in_=b2.partition_broadcast(P))
+
+
 def lay_out_rest(nc, engine, net):
     copy_on(nc, engine, net["b1"][:], net["b1_raw"][:])
     copy_on(nc, engine, net["w2_grouped"][:], net["w2_raw"][:].rearrange("p t c -> p c t"))
-    copy_on(nc, engine, net["b2"][:], net["b2_raw"][:])
 
 
 def quantise_network(nc, net):
@@ -400,7 +402,9 @@ def tile_combnethe_pa_t_kernel(tc, x, W1o, b1o, W2o, b2o, W1f, b1f, W2f, b2f, ou
         nets.append(load_network(nc, keep, "o", W1o, b1o, W2o, b2o))
         load_x(1)
         load_x(2)
+        load_b2(nc, nets[0], b2o)
         nets.append(load_network(nc, keep, "f", W1f, b1f, W2f, b2f))
+        load_b2(nc, nets[1], b2f)
         lay_out_w1(nc, "vector", nets[0], 0, PACK)
 
         for i in range(-5, STEPS + 4):
@@ -446,6 +450,8 @@ def tile_combnethe_pa_t_kernel(tc, x, W1o, b1o, W2o, b2o, W1f, b1f, W2f, b2f, ou
                 quantise_network(nc, nets[0])
             if i == -1 or i == 0:
                 lay_out_w1(nc, "scalar", nets[1], 2 * (i + 1), 2 * (i + 2))
+            if i == -1 or i == 0:
+                copy_on(nc, "scalar", nets[i + 1]["b2"][:], nets[i + 1]["b2_raw"][:])
             if i == 1:
                 lay_out_rest(nc, "scalar", nets[1])
             if i == 3:

@@ -60,12 +60,10 @@ def load_network(nc, keep, net, w1, b1, w2, b2):
     nc.sync.dma_start(out=b1_raw[:], in_=b1.rearrange("(p t) -> p t", t=PACK))
     w2_raw = keep.tile([P, PACK, CLASSES], BF16, name="w2_raw_" + net)
     nc.sync.dma_start(out=w2_raw[:], in_=w2.rearrange("(p t) c -> p t c", t=PACK))
-    b2_raw = keep.tile([P, CLASSES], BF16, name="b2_raw_" + net)
     return {
         "w1_raw": w1_raw,
         "b1_raw": b1_raw,
         "w2_raw": w2_raw,
-        "b2_raw": b2_raw,
         "w1_grouped": keep.tile([P, D_H, PACK], BF16, name="w1_grouped_" + net, align_bytes=64),
         "w2_grouped": keep.tile([P, CLASSES, PACK], BF16, name="w2_grouped_" + net, align_bytes=64),
         "w1": (
@@ -88,10 +86,6 @@ def lay_out_w1(nc, engine, net, first, last):
         net["w1_grouped"][:].rearrange("p (t m) j -> p t m j", t=PACK)[:, first:last],
         net["w1_raw"][:].rearrange("p j (m t) -> p t m j", t=PACK)[:, first:last],
     )
-
-
-def load_b2(nc, net, b2):
-    nc.sync.dma_start(out=net["b2_raw"][:], in_=b2.partition_broadcast(P))
 
 
 def lay_out_rest(nc, engine, net):
@@ -185,6 +179,10 @@ def tile_combnethe_pa_t_kernel(tc, x, W1o, b1o, W2o, b2o, W1f, b1f, W2f, b2f, ou
 
         identity = keep.tile([P, P], F32, name="identity")
         make_identity(nc, identity[:])
+        ones = keep.tile([P, P], BF16, name="ones")
+        nc.gpsimd.memset(ones[:], 1.0)
+        b2_first_row = keep.tile([P, 2 * CLASSES], BF16, name="b2_first_row")
+        nc.gpsimd.memset(b2_first_row[:], 0.0)
         warm = keep.tile([P, 1], F32, name="warm")
         nc.gpsimd.memset(warm[:], 0.0)
         nc.scalar.activation(out=warm[:], in_=warm[:], func=ACT.Exp)
@@ -400,11 +398,11 @@ def tile_combnethe_pa_t_kernel(tc, x, W1o, b1o, W2o, b2o, W1f, b1f, W2f, b2f, ou
 
         load_x(0)
         nets.append(load_network(nc, keep, "o", W1o, b1o, W2o, b2o))
+        nc.sync.dma_start(out=b2_first_row[0:1, 0:CLASSES], in_=b2o.rearrange("(o c) -> o c", o=1))
+        nc.sync.dma_start(out=b2_first_row[0:1, CLASSES:], in_=b2f.rearrange("(o c) -> o c", o=1))
         load_x(1)
         load_x(2)
-        load_b2(nc, nets[0], b2o)
         nets.append(load_network(nc, keep, "f", W1f, b1f, W2f, b2f))
-        load_b2(nc, nets[1], b2f)
         lay_out_w1(nc, "vector", nets[0], 0, PACK)
 
         for i in range(-5, STEPS + 4):
@@ -450,8 +448,18 @@ def tile_combnethe_pa_t_kernel(tc, x, W1o, b1o, W2o, b2o, W1f, b1f, W2f, b2f, ou
                 quantise_network(nc, nets[0])
             if i == -1 or i == 0:
                 lay_out_w1(nc, "scalar", nets[1], 2 * (i + 1), 2 * (i + 2))
-            if i == -1 or i == 0:
-                copy_on(nc, "scalar", nets[i + 1]["b2"][:], nets[i + 1]["b2_raw"][:])
+            if i == -2:
+                b2_spread = psum_l.tile([P, GROUP_TILES, CLASSES], F32, name="acc")
+                nc.tensor.matmul(
+                    out=b2_spread[:, 0:2, :].rearrange("p n c -> p (n c)"),
+                    lhsT=ones[:],
+                    rhs=b2_first_row[:],
+                    start=True,
+                    stop=True,
+                )
+            if i == -1:
+                copy_on(nc, "scalar", nets[0]["b2"][:], b2_spread[:, 0, :])
+                copy_on(nc, "scalar", nets[1]["b2"][:], b2_spread[:, 1, :])
             if i == 1:
                 lay_out_rest(nc, "scalar", nets[1])
             if i == 3:

@@ -25,7 +25,7 @@ HALF_TILES = TILES // 2
 WORDS = D_IN // 2
 TAU = 0.5
 SERIES_STEPS = 3
-SCALAR_X_GROUPS = 2
+VECTOR_X_GROUPS = (2, 3)
 
 FLOPS = 2 * (2 * ROWS * D_IN * D_H + 2 * ROWS * D_H * CLASSES)
 
@@ -93,12 +93,15 @@ def lay_out_rest(nc, engine, net):
     copy_on(nc, engine, net["w2_grouped"][:], net["w2_raw"][:].rearrange("p t c -> p c t"))
 
 
-def quantise_network(nc, net):
+def quantise_w1(nc, net):
     quantise(nc, net["w1_grouped"][:].rearrange("p c j -> p (c j)"), net["w1"][0][:], net["w1"][1][:])
+
+
+def quantise_w2(nc, net):
     quantise(nc, net["w2_grouped"][:].rearrange("p c t -> p (c t)"), net["w2"][0][:], net["w2"][1][:])
 
 
-def gate_slots(nc, gate, sums, half):
+def gate_slots(nc, gate, stats, half):
     cols = slice(half * HALF_TILES, (half + 1) * HALF_TILES)
     tag = "_%d" % half
     slots = []
@@ -119,6 +122,11 @@ def gate_slots(nc, gate, sums, half):
             out=out[:], in0=in0[:], scalar=scalar, in1=in1[:], op0=op0, op1=ALU.mult
         )
 
+    def plus(out, in0, factor, in1):
+        return lambda: nc.vector.scalar_tensor_tensor(
+            out=out[:], in0=in0[:], scalar=factor, in1=in1[:], op0=ALU.mult, op1=ALU.add
+        )
+
     def series(total, factor, shift, name, fill):
         b = [new("b0_" + name), new("b1_" + name)]
         a = new("a_" + name)
@@ -130,30 +138,36 @@ def gate_slots(nc, gate, sums, half):
         return a
 
     c0 = 2.0 / (2.0 + TAU**2)
-    recip1, recip2, recip4, recip8 = new("recip1"), new("recip2"), new("recip4"), new("recip8")
+    mean1, spread1 = stats["e1"][:, cols, 1], stats["e1"][:, cols, 2]
+    mean4, spread4 = stats["e4"][:, cols, 1], stats["e4"][:, cols, 2]
+    n = float(CLASSES)
+    r1, r2, r4, r8 = new("r1"), new("r2"), new("r4"), new("r8")
+    recip1 = new("recip1")
     part0, part1, part2 = new("part0"), new("part1"), new("part2")
-    slots.append([lambda: nc.vector.reciprocal(out=recip1[:], in_=sums["e1"][:, cols])])
-    slots.append([mul(recip2, recip1[:], recip1[:])])
-    slots.append([mul(part0, sums["e2"][:, cols], recip2[:]), mul(recip4, recip2[:], recip2[:])])
+    part1_squared = new("part1_squared")
+    slots.append([lambda: nc.vector.reciprocal(out=r1[:], in_=mean1)])
+    slots.append([mul(r2, r1[:], r1[:]), affine(recip1, r1, 1.0 / n, 0.0)])
+    slots.append([mul(part0, spread1, r2[:]), mul(r4, r2[:], r2[:])])
 
     a0 = series(
         part0,
-        -c0,
-        1.0 - c0 * TAU**2,
+        -c0 / n**2,
+        1.0 - c0 * (TAU**2 + 1.0 / n),
         "0",
-        [mul(part1, sums["e4"][:, cols], recip4[:]), mul(recip8, recip4[:], recip4[:])],
+        [mul(part1, mean4, r4[:]), mul(r8, r4[:], r4[:])],
     )
 
     square0, rest1 = new("square0"), new("rest1")
-    slots.append([mul(square0, a0[:], a0[:]), mul(part2, sums["e8"][:, cols], recip8[:])])
-    slots.append([fused(rest1, part1, TAU**4, ALU.add, square0)])
-    a1 = series(rest1, -(c0**2), 1.0, "1", [])
+    spread4_r8 = new("spread4_r8")
+    slots.append([mul(square0, a0[:], a0[:]), mul(spread4_r8, spread4, r8[:])])
+    slots.append([fused(rest1, part1, TAU**4 * n**3, ALU.add, square0), mul(part1_squared, part1[:], part1[:])])
+    a1 = series(rest1, -(c0**2) / n**3, 1.0, "1", [plus(part2, part1_squared, n, spread4_r8)])
 
     both, square1, rest2 = new("both"), new("square1"), new("rest2")
     slots.append([mul(both, square0[:], a1[:])])
     slots.append([mul(square1, both[:], both[:])])
-    slots.append([fused(rest2, part2, TAU**8, ALU.add, square1)])
-    a2 = series(rest2, -(c0**4), 1.0, "2", [])
+    slots.append([fused(rest2, part2, TAU**8 * n**8, ALU.add, square1)])
+    a2 = series(rest2, -(c0**4) / n**8, 1.0, "2", [])
 
     minus_cond, alpha = new("minus_cond"), new("alpha")
     slots.append([fused(minus_cond, square1, -(TAU**8) * c0**4, ALU.mult, a2)])
@@ -188,13 +202,13 @@ def tile_combnethe_pa_t_kernel(tc, x, W1o, b1o, W2o, b2o, W1f, b1f, W2f, b2f, ou
         nc.scalar.activation(out=warm[:], in_=warm[:], func=ACT.Exp)
 
         nets = []
-        sums = {}
-        for power in ("e1", "e2", "e4", "e8"):
-            sums[power] = gate.tile([P, TILES], F32, name="sum_" + power)
+        stats = {}
+        for power in ("e1", "e4"):
+            stats[power] = gate.tile([P, TILES, 3], F32, name="stats_" + power)
         minus_cond, alpha = [], []
         waiting, issued = [], [0]
         x_sb, x_t, x_grouped, x_q = {}, {}, {}, {}
-        planes, z, h_grouped, h_q, acc, logits, neg_max, e, e_sum, beta = {}, {}, {}, {}, {}, {}, {}, {}, {}, {}
+        planes, z, h_grouped, h_q, acc, logits, neg_max, e, e4, e_sum, beta = {}, {}, {}, {}, {}, {}, {}, {}, {}, {}, {}
 
         def load_x(g):
             x_sb[g] = three.tile([P, GROUP_TILES * D_IN], BF16, name="x_sb")
@@ -220,10 +234,10 @@ def tile_combnethe_pa_t_kernel(tc, x, W1o, b1o, W2o, b2o, W1f, b1f, W2f, b2f, ou
             grouped_words = x_grouped[g][:].bitcast(F32)
             out = grouped_words[:, half * 2 * WORDS : (half + 1) * 2 * WORDS].rearrange("p (j r u) -> p j r u", j=2, u=2)
             in_ = x_t[g][half][:].rearrange("p j u r -> p j r u")
-            if g < SCALAR_X_GROUPS:
-                nc.scalar.copy(out=out, in_=in_)
-            else:
+            if g in VECTOR_X_GROUPS:
                 nc.vector.tensor_copy(out=out, in_=in_)
+            else:
+                nc.scalar.copy(out=out, in_=in_)
 
         def quantise_x(g):
             x_q[g] = (
@@ -231,13 +245,6 @@ def tile_combnethe_pa_t_kernel(tc, x, W1o, b1o, W2o, b2o, W1f, b1f, W2f, b2f, ou
                 keep.tile([P, GROUP_ROWS], U8, name="x_scales_%d" % g, align_bytes=64),
             )
             quantise(nc, x_grouped[g][:], x_q[g][0][:], x_q[g][1][:])
-
-        def vector_banks(s):
-            if GROUPS - 2 <= s < GROUPS + 3:
-                return 2
-            if 0 <= s < GROUPS and (s % 4 == 3 or s == GROUPS - 3):
-                return 1
-            return 0
 
         def hidden_product(s, t):
             if s < STEPS:
@@ -251,30 +258,14 @@ def tile_combnethe_pa_t_kernel(tc, x, W1o, b1o, W2o, b2o, W1f, b1f, W2f, b2f, ou
             if s >= 0:
                 planes[s] = two.tile([P, PACK, GROUP_ROWS], BF16, name="planes")
             for t in range(PACK):
-                if t < PACK - vector_banks(s):
-                    if s >= 0:
-                        nc.scalar.activation(
-                            out=planes[s][:, t, :],
-                            in_=z[(s, t)][:],
-                            func=ACT.Relu,
-                            bias=nets[s // GROUPS]["b1"][:, t : t + 1],
-                            scale=1.0,
-                        )
-                    hidden_product(s + 1, t)
-
-        def vector_relu(s):
-            for t in range(PACK - vector_banks(s), PACK):
-                nc.vector.tensor_scalar(
-                    out=planes[s][:, t, :],
-                    in0=z[(s, t)][:],
-                    scalar1=nets[s // GROUPS]["b1"][:, t : t + 1],
-                    scalar2=0.0,
-                    op0=ALU.add,
-                    op1=ALU.max,
-                )
-
-        def last_product(s):
-            for t in range(PACK - vector_banks(s), PACK):
+                if s >= 0:
+                    nc.scalar.activation(
+                        out=planes[s][:, t, :],
+                        in_=z[(s, t)][:],
+                        func=ACT.Relu,
+                        bias=nets[s // GROUPS]["b1"][:, t : t + 1],
+                        scale=1.0,
+                    )
                 hidden_product(s + 1, t)
 
         def regroup_h(s):
@@ -314,33 +305,41 @@ def tile_combnethe_pa_t_kernel(tc, x, W1o, b1o, W2o, b2o, W1f, b1f, W2f, b2f, ou
         def exponentials(s):
             if s < GROUPS:
                 e[s] = keep.tile([P, GROUP_TILES, CLASSES], F32, name="e_o_%d" % s)
-                e_sum[s] = sums["e1"][:, s * GROUP_TILES : (s + 1) * GROUP_TILES]
+                e4[s] = two.tile([P, GROUP_TILES, CLASSES], F32, name="e4")
+                neg_max4 = two.tile([P, GROUP_TILES], F32, name="neg_max4")
+                nc.scalar.activation(out=neg_max4[:], in_=neg_max[s][:], func=ACT.Copy, scale=4.0)
+                for j in range(GROUP_TILES):
+                    nc.scalar.activation(
+                        out=e[s][:, j, :], in_=logits[s][:, j, :], func=ACT.Exp, bias=neg_max[s][:, j : j + 1], scale=1.0
+                    )
+                for j in range(GROUP_TILES):
+                    nc.scalar.activation(
+                        out=e4[s][:, j, :], in_=logits[s][:, j, :], func=ACT.Exp, bias=neg_max4[:, j : j + 1], scale=4.0
+                    )
             else:
                 e[s] = five.tile([P, GROUP_TILES, CLASSES], F32, name="e_f")
                 e_sum[s] = three.tile([P, GROUP_TILES], F32, name="sum_f")
-            for j in range(GROUP_TILES):
-                nc.scalar.activation(
-                    out=e[s][:, j, :],
-                    in_=logits[s][:, j, :],
-                    func=ACT.Exp,
-                    bias=neg_max[s][:, j : j + 1],
-                    scale=1.0,
-                    accum_out=e_sum[s][:, j : j + 1],
-                )
-
-        def power_sums(s):
-            powers = two.tile([P, GROUP_TILES, CLASSES], F32, name="powers")
-            for power in ("e2", "e4", "e8"):
                 for j in range(GROUP_TILES):
                     nc.scalar.activation(
-                        out=powers[:, j, :],
-                        in_=e[s][:, j, :] if power == "e2" else powers[:, j, :],
-                        func=ACT.Square,
-                        accum_out=sums[power][:, s * GROUP_TILES + j : s * GROUP_TILES + j + 1],
+                        out=e[s][:, j, :],
+                        in_=logits[s][:, j, :],
+                        func=ACT.Exp,
+                        bias=neg_max[s][:, j : j + 1],
+                        scale=1.0,
+                        accum_out=e_sum[s][:, j : j + 1],
                     )
 
+        def statistics(s, power):
+            values = {"e1": e, "e4": e4}[power][s]
+            for half in range(2):
+                j = s * GROUP_TILES + 2 * half
+                nc.vector.bn_stats(
+                    out=stats[power][:, j : j + 2, :].rearrange("p j k -> p (j k)"),
+                    in_=values[:, 2 * half : 2 * half + 2, :].rearrange("p j c -> p c j"),
+                )
+
         def gate_half(half):
-            slots, minus_cond_half, alpha_half = gate_slots(nc, gate, sums, half)
+            slots, minus_cond_half, alpha_half = gate_slots(nc, gate, stats, half)
             waiting.extend(slots)
             minus_cond.append(minus_cond_half)
             alpha.append(alpha_half)
@@ -407,45 +406,40 @@ def tile_combnethe_pa_t_kernel(tc, x, W1o, b1o, W2o, b2o, W1f, b1f, W2f, b2f, ou
 
         for i in range(-5, STEPS + 4):
             run(load_x, i + 5, 3, GROUPS)
-            if i + 3 < SCALAR_X_GROUPS:
+            run(regroup_h, i, 0, STEPS)
+            gate_slot()
+            run(quantise_x, i + 2, 0, GROUPS)
+            run(hidden_layer, i + 1, -1, STEPS)
+            if i + 3 not in VECTOR_X_GROUPS:
                 run(lambda g: copy_x_out(g, 0), i + 3, 0, GROUPS)
                 run(lambda g: copy_x_out(g, 1), i + 3, 0, GROUPS)
             if i == -3:
                 lay_out_rest(nc, "scalar", nets[0])
-            run(hidden_layer, i + 1, -1, STEPS)
-            run(regroup_h, i, 0, STEPS)
+                quantise_w1(nc, nets[0])
+            if i == -1:
+                quantise_w2(nc, nets[0])
+            run(lambda s: statistics(s, "e1"), i - 3, 0, GROUPS)
+            run(blend_reciprocal, i - 3, GROUPS, STEPS)
+            if i + 2 >= GROUPS:
+                run(add_bias, i - 1, 0, STEPS)
+                gate_slot()
+            run(quantise_h, i, 0, STEPS)
             gate_slot()
-            if i + 3 < GROUPS:
-                run(lambda g: copy_x_out(g, 0), i + 3, SCALAR_X_GROUPS, GROUPS)
-                run(quantise_h, i, 0, STEPS)
-                gate_slot()
-                run(lambda g: copy_x_out(g, 1), i + 3, SCALAR_X_GROUPS, GROUPS)
-                run(vector_relu, i + 1, 0, STEPS)
-                run(transpose_x, i + 4, 0, GROUPS)
-                run(head, i, 0, STEPS)
-                run(last_product, i + 1, 0, STEPS)
+            run(head, i, 0, STEPS)
+            if i + 3 in VECTOR_X_GROUPS:
+                copy_x_out(i + 3, 0)
+                copy_x_out(i + 3, 1)
+            run(transpose_x, i + 4, 0, GROUPS)
+            if i + 2 < GROUPS:
                 run(add_bias, i - 1, 0, STEPS)
                 gate_slot()
-                run(quantise_x, i + 3, 0, GROUPS)
-                run(row_max, i - 1, 0, STEPS)
-            else:
-                run(blend_reciprocal, i - 3, GROUPS, STEPS)
-                run(add_bias, i - 1, 0, STEPS)
-                gate_slot()
-                run(quantise_h, i, 0, STEPS)
-                gate_slot()
-                run(vector_relu, i + 1, 0, STEPS)
-                run(head, i, 0, STEPS)
-                run(last_product, i + 1, 0, STEPS)
-                run(blend_beta, i - 3, GROUPS, STEPS)
-                run(row_max, i - 1, 0, STEPS)
+            run(lambda s: statistics(s, "e4"), i - 3, 0, GROUPS)
+            run(blend_beta, i - 3, GROUPS, STEPS)
+            run(row_max, i - 1, 0, STEPS)
             gate_slot()
             run(exponentials, i - 2, 0, STEPS)
-            run(power_sums, i - 2, 0, GROUPS)
             run(blend_scale_o, i - 2, GROUPS, STEPS)
             run(blend_and_store, i - 3, GROUPS, STEPS)
-            if i == -3:
-                quantise_network(nc, nets[0])
             if i == -1 or i == 0:
                 lay_out_w1(nc, "scalar", nets[1], 2 * (i + 1), 2 * (i + 2))
             if i == -2:
@@ -463,7 +457,8 @@ def tile_combnethe_pa_t_kernel(tc, x, W1o, b1o, W2o, b2o, W1f, b1f, W2f, b2f, ou
             if i == 1:
                 lay_out_rest(nc, "scalar", nets[1])
             if i == 3:
-                quantise_network(nc, nets[1])
+                quantise_w1(nc, nets[1])
+                quantise_w2(nc, nets[1])
             if i - 3 in (HALF_GROUPS - 1, GROUPS - 1):
                 assert issued[0] == len(waiting)
                 gate_half((i - 3) // HALF_GROUPS)

@@ -75,7 +75,7 @@ def load_network(nc, keep, net, w1, b1, w2, b2):
             keep.tile([P, CLASSES], U8, name="w2_scales_" + net, align_bytes=64),
         ),
         "b1": keep.tile([P, PACK], F32, name="b1_cols_" + net),
-        "b2": keep.tile([P, CLASSES], F32, name="b2_rows_" + net),
+        "b2": keep.tile([P, CLASSES if net == "o" else 1], F32, name="b2_" + net),
     }
 
 
@@ -210,6 +210,10 @@ def tile_combnethe_pa_t_kernel(tc, x, W1o, b1o, W2o, b2o, W1f, b1f, W2f, b2f, ou
         x_sb, x_t, x_grouped, x_q = {}, {}, {}, {}
         planes, z, h_grouped, h_q, acc, logits, neg_max, e, e4, e_sum, beta = {}, {}, {}, {}, {}, {}, {}, {}, {}, {}, {}
 
+        def run(stage, index, first, last):
+            if first <= index < last:
+                stage(index)
+
         def load_x(g):
             x_sb[g] = three.tile([P, GROUP_TILES * D_IN], BF16, name="x_sb")
             nc.sync.dma_start(
@@ -255,10 +259,12 @@ def tile_combnethe_pa_t_kernel(tc, x, W1o, b1o, W2o, b2o, W1f, b1f, W2f, b2f, ou
                 mx_pass(nc, z[(s, t)][:], (codes[:, cols], scales[:, cols]), (rows[0][:], rows[1][:]))
 
         def hidden_layer(s):
-            if s >= 0:
+            if 0 <= s < STEPS:
                 planes[s] = two.tile([P, PACK, GROUP_ROWS], BF16, name="planes")
             for t in range(PACK):
-                if s >= 0:
+                if t == PACK // 2:
+                    run(turn_logits, s - 2, GROUPS, STEPS)
+                if 0 <= s < STEPS:
                     nc.scalar.activation(
                         out=planes[s][:, t, :],
                         in_=z[(s, t)][:],
@@ -285,6 +291,9 @@ def tile_combnethe_pa_t_kernel(tc, x, W1o, b1o, W2o, b2o, W1f, b1f, W2f, b2f, ou
         def head(s):
             w2 = nets[s // GROUPS]["w2"]
             acc[s] = psum_l.tile([P, GROUP_TILES, CLASSES], F32, name="acc")
+            if s >= GROUPS:
+                mx_pass(nc, acc[s][:].rearrange("p j r -> p (j r)"), (w2[0][:], w2[1][:]), (h_q[s][0][:], h_q[s][1][:]))
+                return
             for j in range(GROUP_TILES):
                 cols = slice(j * P, (j + 1) * P)
                 mx_pass(nc, acc[s][:, j, :], (h_q[s][0][:, cols], h_q[s][1][:, cols]), (w2[0][:], w2[1][:]))
@@ -297,6 +306,13 @@ def tile_combnethe_pa_t_kernel(tc, x, W1o, b1o, W2o, b2o, W1f, b1f, W2f, b2f, ou
                 in1=nets[s // GROUPS]["b2"][:].unsqueeze(1).to_broadcast([P, GROUP_TILES, CLASSES]),
                 op=ALU.add,
             )
+
+        def turn_logits(s):
+            class_rows = two.tile([P, GROUP_TILES, P], F32, name="class_rows")
+            nc.scalar.activation(out=class_rows[:], in_=acc[s][:], func=ACT.Identity, bias=nets[1]["b2"][:, 0:1], scale=1.0)
+            logits[s] = psum_x.tile([P, GROUP_TILES, CLASSES], F32, name="x_t")
+            for j in range(GROUP_TILES):
+                nc.tensor.transpose(logits[s][:, j, :], class_rows[:, j, :], identity[:])
 
         def row_max(s):
             neg_max[s] = three.tile([P, GROUP_TILES], F32, name="neg_max")
@@ -355,11 +371,12 @@ def tile_combnethe_pa_t_kernel(tc, x, W1o, b1o, W2o, b2o, W1f, b1f, W2f, b2f, ou
             assert issued[0] == len(waiting) or g % HALF_GROUPS > 0
             for j in range(GROUP_TILES):
                 column = (g % HALF_GROUPS) * GROUP_TILES + j
-                nc.scalar.activation(
+                nc.vector.tensor_scalar(
                     out=e[g][:, j, :],
-                    in_=e[g][:, j, :],
-                    func=ACT.Copy,
-                    scale=alpha[g // HALF_GROUPS][:, column : column + 1],
+                    in0=e[g][:, j, :],
+                    scalar1=alpha[g // HALF_GROUPS][:, column : column + 1],
+                    scalar2=None,
+                    op0=ALU.mult,
                 )
 
         def blend_reciprocal(s):
@@ -391,10 +408,6 @@ def tile_combnethe_pa_t_kernel(tc, x, W1o, b1o, W2o, b2o, W1f, b1f, W2f, b2f, ou
                 )
             nc.sync.dma_start(out=out_rows[:, g * GROUP_TILES : (g + 1) * GROUP_TILES, :], in_=e[s][:])
 
-        def run(stage, index, first, last):
-            if first <= index < last:
-                stage(index)
-
         load_x(0)
         nets.append(load_network(nc, keep, "o", W1o, b1o, W2o, b2o))
         nc.sync.dma_start(out=b2_first_row[0:1, 0:CLASSES], in_=b2o.rearrange("(o c) -> o c", o=1))
@@ -409,7 +422,7 @@ def tile_combnethe_pa_t_kernel(tc, x, W1o, b1o, W2o, b2o, W1f, b1f, W2f, b2f, ou
             run(regroup_h, i, 0, STEPS)
             gate_slot()
             run(quantise_x, i + 2, 0, GROUPS)
-            run(hidden_layer, i + 1, -1, STEPS)
+            run(hidden_layer, i + 1, -1, STEPS + 2)
             if i + 3 not in VECTOR_X_GROUPS:
                 run(lambda g: copy_x_out(g, 0), i + 3, 0, GROUPS)
                 run(lambda g: copy_x_out(g, 1), i + 3, 0, GROUPS)
@@ -421,7 +434,8 @@ def tile_combnethe_pa_t_kernel(tc, x, W1o, b1o, W2o, b2o, W1f, b1f, W2f, b2f, ou
             run(lambda s: statistics(s, "e1"), i - 3, 0, GROUPS)
             run(blend_reciprocal, i - 3, GROUPS, STEPS)
             if i + 2 >= GROUPS:
-                run(add_bias, i - 1, 0, STEPS)
+                run(add_bias, i - 1, 0, GROUPS)
+                run(blend_scale_o, i - 2, GROUPS, STEPS)
                 gate_slot()
             run(quantise_h, i, 0, STEPS)
             gate_slot()
@@ -438,22 +452,16 @@ def tile_combnethe_pa_t_kernel(tc, x, W1o, b1o, W2o, b2o, W1f, b1f, W2f, b2f, ou
             run(row_max, i - 1, 0, STEPS)
             gate_slot()
             run(exponentials, i - 2, 0, STEPS)
-            run(blend_scale_o, i - 2, GROUPS, STEPS)
             run(blend_and_store, i - 3, GROUPS, STEPS)
             if i == -1 or i == 0:
                 lay_out_w1(nc, "scalar", nets[1], 2 * (i + 1), 2 * (i + 2))
             if i == -2:
                 b2_spread = psum_l.tile([P, GROUP_TILES, CLASSES], F32, name="acc")
-                nc.tensor.matmul(
-                    out=b2_spread[:, 0:2, :].rearrange("p n c -> p (n c)"),
-                    lhsT=ones[:],
-                    rhs=b2_first_row[:],
-                    start=True,
-                    stop=True,
-                )
+                nc.tensor.matmul(out=b2_spread[:, 0, :], lhsT=ones[:], rhs=b2_first_row[:, 0:CLASSES], start=True, stop=True)
+                nc.tensor.matmul(out=b2_spread[:, 1, :], lhsT=b2_first_row[:, CLASSES:], rhs=ones[:], start=True, stop=True)
             if i == -1:
                 copy_on(nc, "scalar", nets[0]["b2"][:], b2_spread[:, 0, :])
-                copy_on(nc, "scalar", nets[1]["b2"][:], b2_spread[:, 1, :])
+                copy_on(nc, "scalar", nets[1]["b2"][:], b2_spread[:, 1, 0:1])
             if i == 1:
                 lay_out_rest(nc, "scalar", nets[1])
             if i == 3:

@@ -22,10 +22,20 @@ GROUPS = TILES // GROUP_TILES
 STEPS = 2 * GROUPS
 HALF_GROUPS = GROUPS // 2
 HALF_TILES = TILES // 2
+HALVES = ((0, GROUP_TILES // 2), (GROUP_TILES // 2, GROUP_TILES))
+PIECES = (
+    [(0, first, last) for first, last in HALVES]
+    + [(step, 0, GROUP_TILES) for step in range(1, STEPS - 1)]
+    + [(STEPS - 1, first, last) for first, last in HALVES]
+)
+COUNT = len(PIECES)
+O_COUNT = GROUPS + 1
+TURNED = range(O_COUNT, COUNT - 2)
+SCALAR_SCALED = range(COUNT - 3, COUNT)
 WORDS = D_IN // 2
 TAU = 0.5
 SERIES_STEPS = 3
-VECTOR_X_GROUPS = (2, 3)
+VECTOR_X_PIECES = (3, 4)
 
 FLOPS = 2 * (2 * ROWS * D_IN * D_H + 2 * ROWS * D_H * CLASSES)
 
@@ -75,7 +85,8 @@ def load_network(nc, keep, net, w1, b1, w2, b2):
             keep.tile([P, CLASSES], U8, name="w2_scales_" + net, align_bytes=64),
         ),
         "b1": keep.tile([P, PACK], F32, name="b1_cols_" + net),
-        "b2": keep.tile([P, CLASSES if net == "o" else 1], F32, name="b2_" + net),
+        "b2_row": keep.tile([P, CLASSES], F32, name="b2_row_" + net),
+        "b2_col": keep.tile([P, 1], F32, name="b2_col_" + net),
     }
 
 
@@ -93,8 +104,9 @@ def lay_out_rest(nc, engine, net):
     copy_on(nc, engine, net["w2_grouped"][:], net["w2_raw"][:].rearrange("p t c -> p c t"))
 
 
-def quantise_w1(nc, net):
-    quantise(nc, net["w1_grouped"][:].rearrange("p c j -> p (c j)"), net["w1"][0][:], net["w1"][1][:])
+def quantise_w1(nc, net, first, last):
+    cols = slice(first * P, last * P)
+    quantise(nc, net["w1_grouped"][:, cols, :].rearrange("p c j -> p (c j)"), net["w1"][0][:, cols], net["w1"][1][:, cols])
 
 
 def quantise_w2(nc, net):
@@ -214,144 +226,172 @@ def tile_combnethe_pa_t_kernel(tc, x, W1o, b1o, W2o, b2o, W1f, b1f, W2f, b2f, ou
             if first <= index < last:
                 stage(index)
 
-        def load_x(g):
-            x_sb[g] = three.tile([P, GROUP_TILES * D_IN], BF16, name="x_sb")
+        def rows_of(k):
+            return slice(PIECES[k][1] * P, PIECES[k][2] * P)
+
+        def width(k):
+            return (PIECES[k][2] - PIECES[k][1]) * P
+
+        def net_of(k):
+            return nets[PIECES[k][0] // GROUPS]
+
+        def load_x(k):
+            g, first, last = PIECES[k]
+            x_sb[k] = three.tile([P, GROUP_TILES * D_IN], BF16, name="x_sb")
             nc.sync.dma_start(
-                out=x_sb[g][:].rearrange("p (j k) -> p j k", j=GROUP_TILES),
-                in_=x_rows[:, g * GROUP_TILES : (g + 1) * GROUP_TILES, :],
+                out=x_sb[k][:, : (last - first) * D_IN].rearrange("p (j k) -> p j k", j=last - first),
+                in_=x_rows[:, g * GROUP_TILES + first : g * GROUP_TILES + last, :],
             )
 
-        def transpose_x(g):
-            x_words = x_sb[g][:].bitcast(F32)
-            x_t[g] = []
-            for half in range(2):
+        def transpose_x(k):
+            x_words = x_sb[k][:].bitcast(F32)
+            x_t[k] = []
+            for pair in range(width(k) // (2 * P)):
                 bank = psum_x.tile([P, 2, 2, P], F32, name="x_t")
                 for jj in range(2):
                     for u in range(2):
-                        first = (2 * half + jj) * WORDS
-                        nc.tensor.transpose(bank[:, jj, u, :], x_words[:, first + u : first + WORDS : 2], identity[:])
-                x_t[g].append(bank)
+                        start = (2 * pair + jj) * WORDS
+                        nc.tensor.transpose(bank[:, jj, u, :], x_words[:, start + u : start + WORDS : 2], identity[:])
+                x_t[k].append(bank)
 
-        def copy_x_out(g, half):
-            if half == 0:
-                x_grouped[g] = two.tile([P, GROUP_ROWS * PACK], BF16, name="x_grouped", align_bytes=64)
-            grouped_words = x_grouped[g][:].bitcast(F32)
-            out = grouped_words[:, half * 2 * WORDS : (half + 1) * 2 * WORDS].rearrange("p (j r u) -> p j r u", j=2, u=2)
-            in_ = x_t[g][half][:].rearrange("p j u r -> p j r u")
-            if g in VECTOR_X_GROUPS:
-                nc.vector.tensor_copy(out=out, in_=in_)
-            else:
-                nc.scalar.copy(out=out, in_=in_)
+        def copy_x_out(k):
+            x_grouped[k] = two.tile([P, GROUP_ROWS * PACK], BF16, name="x_grouped", align_bytes=64)
+            grouped_words = x_grouped[k][:].bitcast(F32)
+            for pair, bank in enumerate(x_t[k]):
+                out = grouped_words[:, pair * 2 * WORDS : (pair + 1) * 2 * WORDS].rearrange("p (j r u) -> p j r u", j=2, u=2)
+                in_ = bank[:].rearrange("p j u r -> p j r u")
+                if k in VECTOR_X_PIECES:
+                    nc.vector.tensor_copy(out=out, in_=in_)
+                else:
+                    nc.scalar.copy(out=out, in_=in_)
 
-        def quantise_x(g):
-            x_q[g] = (
-                keep.tile([P, GROUP_ROWS], U32, name="x_codes_%d" % g, align_bytes=64),
-                keep.tile([P, GROUP_ROWS], U8, name="x_scales_%d" % g, align_bytes=64),
-            )
-            quantise(nc, x_grouped[g][:], x_q[g][0][:], x_q[g][1][:])
+        def quantise_x(k):
+            g, first, last = PIECES[k]
+            if first == 0:
+                x_q[g] = (
+                    keep.tile([P, GROUP_ROWS], U32, name="x_codes_%d" % g, align_bytes=64),
+                    keep.tile([P, GROUP_ROWS], U8, name="x_scales_%d" % g, align_bytes=64),
+                )
+            quantise(nc, x_grouped[k][:, : width(k) * PACK], x_q[g][0][:, rows_of(k)], x_q[g][1][:, rows_of(k)])
 
-        def hidden_product(s, t):
-            if s < STEPS:
-                codes, scales = nets[s // GROUPS]["w1"]
-                rows = x_q[s % GROUPS]
-                z[(s, t)] = psum_z.tile([P, GROUP_ROWS], F32, name="z")
+        def hidden_product(k, t):
+            if k < COUNT:
+                codes, scales = net_of(k)["w1"]
+                rows = x_q[PIECES[k][0] % GROUPS]
+                z[(k, t)] = psum_z.tile([P, GROUP_ROWS], F32, name="z")
                 cols = slice(t * P, (t + 1) * P)
-                mx_pass(nc, z[(s, t)][:], (codes[:, cols], scales[:, cols]), (rows[0][:], rows[1][:]))
+                mx_pass(
+                    nc,
+                    z[(k, t)][:, : width(k)],
+                    (codes[:, cols], scales[:, cols]),
+                    (rows[0][:, rows_of(k)], rows[1][:, rows_of(k)]),
+                )
 
-        def hidden_layer(s):
-            if 0 <= s < STEPS:
-                planes[s] = two.tile([P, PACK, GROUP_ROWS], BF16, name="planes")
+        def hidden_layer(k):
+            if 0 <= k < COUNT:
+                planes[k] = two.tile([P, PACK, GROUP_ROWS], BF16, name="planes")
             for t in range(PACK):
-                if t == PACK // 2:
-                    run(turn_logits, s - 2, GROUPS, STEPS)
-                if 0 <= s < STEPS:
+                if t == PACK // 2 and k - 2 in TURNED:
+                    turn_logits(k - 2)
+                if 0 <= k < COUNT:
                     nc.scalar.activation(
-                        out=planes[s][:, t, :],
-                        in_=z[(s, t)][:],
+                        out=planes[k][:, t, : width(k)],
+                        in_=z[(k, t)][:, : width(k)],
                         func=ACT.Relu,
-                        bias=nets[s // GROUPS]["b1"][:, t : t + 1],
+                        bias=net_of(k)["b1"][:, t : t + 1],
                         scale=1.0,
                     )
-                hidden_product(s + 1, t)
+                hidden_product(k + 1, t)
 
-        def regroup_h(s):
-            h_grouped[s] = two.tile([P, GROUP_ROWS, PACK], BF16, name="h_grouped", align_bytes=64)
+        def regroup_h(k):
+            h_grouped[k] = two.tile([P, GROUP_ROWS, PACK], BF16, name="h_grouped", align_bytes=64)
             nc.vector.tensor_copy(
-                out=h_grouped[s][:].rearrange("p (c i) t -> p c t i", i=4),
-                in_=planes[s][:].rearrange("p t (c i) -> p c t i", i=4),
+                out=h_grouped[k][:, : width(k), :].rearrange("p (c i) t -> p c t i", i=4),
+                in_=planes[k][:, :, : width(k)].rearrange("p t (c i) -> p c t i", i=4),
             )
 
-        def quantise_h(s):
-            h_q[s] = (
+        def quantise_h(k):
+            h_q[k] = (
                 two.tile([P, GROUP_ROWS], U32, name="h_codes", align_bytes=64),
                 two.tile([P, GROUP_ROWS], U8, name="h_scales", align_bytes=64),
             )
-            quantise(nc, h_grouped[s][:].rearrange("p r t -> p (r t)"), h_q[s][0][:], h_q[s][1][:])
+            n = width(k)
+            quantise(nc, h_grouped[k][:, :n, :].rearrange("p r t -> p (r t)"), h_q[k][0][:, :n], h_q[k][1][:, :n])
 
-        def head(s):
-            w2 = nets[s // GROUPS]["w2"]
-            acc[s] = psum_l.tile([P, GROUP_TILES, CLASSES], F32, name="acc")
-            if s >= GROUPS:
-                mx_pass(nc, acc[s][:].rearrange("p j r -> p (j r)"), (w2[0][:], w2[1][:]), (h_q[s][0][:], h_q[s][1][:]))
+        def head(k):
+            w2 = net_of(k)["w2"]
+            acc[k] = psum_l.tile([P, GROUP_TILES, CLASSES], F32, name="acc")
+            if k in TURNED:
+                mx_pass(nc, acc[k][:].rearrange("p j r -> p (j r)"), (w2[0][:], w2[1][:]), (h_q[k][0][:], h_q[k][1][:]))
+            else:
+                for j in range(width(k) // P):
+                    cols = slice(j * P, (j + 1) * P)
+                    mx_pass(nc, acc[k][:, j, :], (h_q[k][0][:, cols], h_q[k][1][:, cols]), (w2[0][:], w2[1][:]))
+
+        def add_bias(k):
+            if k in TURNED:
                 return
-            for j in range(GROUP_TILES):
-                cols = slice(j * P, (j + 1) * P)
-                mx_pass(nc, acc[s][:, j, :], (h_q[s][0][:, cols], h_q[s][1][:, cols]), (w2[0][:], w2[1][:]))
-
-        def add_bias(s):
-            logits[s] = three.tile([P, GROUP_TILES, CLASSES], F32, name="logits")
+            n = width(k) // P
+            logits[k] = three.tile([P, GROUP_TILES, CLASSES], F32, name="logits")
             nc.vector.tensor_tensor(
-                out=logits[s][:],
-                in0=acc[s][:],
-                in1=nets[s // GROUPS]["b2"][:].unsqueeze(1).to_broadcast([P, GROUP_TILES, CLASSES]),
+                out=logits[k][:, :n, :],
+                in0=acc[k][:, :n, :],
+                in1=net_of(k)["b2_row"][:].unsqueeze(1).to_broadcast([P, n, CLASSES]),
                 op=ALU.add,
             )
 
-        def turn_logits(s):
+        def turn_logits(k):
             class_rows = two.tile([P, GROUP_TILES, P], F32, name="class_rows")
-            nc.scalar.activation(out=class_rows[:], in_=acc[s][:], func=ACT.Identity, bias=nets[1]["b2"][:, 0:1], scale=1.0)
-            logits[s] = psum_x.tile([P, GROUP_TILES, CLASSES], F32, name="x_t")
+            nc.scalar.activation(
+                out=class_rows[:], in_=acc[k][:], func=ACT.Identity, bias=net_of(k)["b2_col"][:, 0:1], scale=1.0
+            )
+            logits[k] = psum_x.tile([P, GROUP_TILES, CLASSES], F32, name="x_t")
             for j in range(GROUP_TILES):
-                nc.tensor.transpose(logits[s][:, j, :], class_rows[:, j, :], identity[:])
+                nc.tensor.transpose(logits[k][:, j, :], class_rows[:, j, :], identity[:])
 
-        def row_max(s):
-            neg_max[s] = three.tile([P, GROUP_TILES], F32, name="neg_max")
-            nc.vector.tensor_reduce(out=neg_max[s][:], in_=logits[s][:], axis=AXIS.X, op=ALU.max, negate=True)
+        def row_max(k):
+            n = width(k) // P
+            neg_max[k] = three.tile([P, GROUP_TILES], F32, name="neg_max")
+            nc.vector.tensor_reduce(
+                out=neg_max[k][:, :n], in_=logits[k][:, :n, :], axis=AXIS.X, op=ALU.max, negate=True
+            )
 
-        def exponentials(s):
-            if s < GROUPS:
-                e[s] = keep.tile([P, GROUP_TILES, CLASSES], F32, name="e_o_%d" % s)
-                e4[s] = two.tile([P, GROUP_TILES, CLASSES], F32, name="e4")
+        def exponentials(k):
+            n = width(k) // P
+            if k < O_COUNT:
+                e[k] = keep.tile([P, n, CLASSES], F32, name="e_o_%d" % k)
+                e4[k] = two.tile([P, GROUP_TILES, CLASSES], F32, name="e4")
                 neg_max4 = two.tile([P, GROUP_TILES], F32, name="neg_max4")
-                nc.scalar.activation(out=neg_max4[:], in_=neg_max[s][:], func=ACT.Copy, scale=4.0)
-                for j in range(GROUP_TILES):
+                nc.scalar.activation(out=neg_max4[:, :n], in_=neg_max[k][:, :n], func=ACT.Copy, scale=4.0)
+                for j in range(n):
                     nc.scalar.activation(
-                        out=e[s][:, j, :], in_=logits[s][:, j, :], func=ACT.Exp, bias=neg_max[s][:, j : j + 1], scale=1.0
+                        out=e[k][:, j, :], in_=logits[k][:, j, :], func=ACT.Exp, bias=neg_max[k][:, j : j + 1], scale=1.0
                     )
-                for j in range(GROUP_TILES):
+                for j in range(n):
                     nc.scalar.activation(
-                        out=e4[s][:, j, :], in_=logits[s][:, j, :], func=ACT.Exp, bias=neg_max4[:, j : j + 1], scale=4.0
+                        out=e4[k][:, j, :], in_=logits[k][:, j, :], func=ACT.Exp, bias=neg_max4[:, j : j + 1], scale=4.0
                     )
             else:
-                e[s] = five.tile([P, GROUP_TILES, CLASSES], F32, name="e_f")
-                e_sum[s] = three.tile([P, GROUP_TILES], F32, name="sum_f")
-                for j in range(GROUP_TILES):
+                e[k] = five.tile([P, GROUP_TILES, CLASSES], F32, name="e_f")
+                e_sum[k] = three.tile([P, GROUP_TILES], F32, name="sum_f")
+                for j in range(n):
                     nc.scalar.activation(
-                        out=e[s][:, j, :],
-                        in_=logits[s][:, j, :],
+                        out=e[k][:, j, :],
+                        in_=logits[k][:, j, :],
                         func=ACT.Exp,
-                        bias=neg_max[s][:, j : j + 1],
+                        bias=neg_max[k][:, j : j + 1],
                         scale=1.0,
-                        accum_out=e_sum[s][:, j : j + 1],
+                        accum_out=e_sum[k][:, j : j + 1],
                     )
 
-        def statistics(s, power):
-            values = {"e1": e, "e4": e4}[power][s]
-            for half in range(2):
-                j = s * GROUP_TILES + 2 * half
+        def statistics(k, power):
+            g, first, last = PIECES[k]
+            values = {"e1": e, "e4": e4}[power][k]
+            for j in range(0, last - first, 2):
+                tile = g * GROUP_TILES + first + j
                 nc.vector.bn_stats(
-                    out=stats[power][:, j : j + 2, :].rearrange("p j k -> p (j k)"),
-                    in_=values[:, 2 * half : 2 * half + 2, :].rearrange("p j c -> p c j"),
+                    out=stats[power][:, tile : tile + 2, :].rearrange("p j k -> p (j k)"),
+                    in_=values[:, j : j + 2, :].rearrange("p j c -> p c j"),
                 )
 
         def gate_half(half):
@@ -366,107 +406,123 @@ def tile_combnethe_pa_t_kernel(tc, x, W1o, b1o, W2o, b2o, W1f, b1f, W2f, b2f, ou
                     instruction()
                 issued[0] += 1
 
-        def blend_scale_o(s):
-            g = s - GROUPS
+        def e_o(k, j):
+            g, tile = PIECES[k][0] - GROUPS, PIECES[k][1] + j
+            for other, (step, first, last) in enumerate(PIECES[:O_COUNT]):
+                if step == g and first <= tile < last:
+                    return e[other][:, tile - first, :]
+
+        def blend_scale_o(k):
+            g, first, last = PIECES[k]
+            g -= GROUPS
             assert issued[0] == len(waiting) or g % HALF_GROUPS > 0
-            for j in range(GROUP_TILES):
-                column = (g % HALF_GROUPS) * GROUP_TILES + j
-                nc.vector.tensor_scalar(
-                    out=e[g][:, j, :],
-                    in0=e[g][:, j, :],
-                    scalar1=alpha[g // HALF_GROUPS][:, column : column + 1],
-                    scalar2=None,
-                    op0=ALU.mult,
-                )
+            for j in range(last - first):
+                column = (g % HALF_GROUPS) * GROUP_TILES + first + j
+                factor = alpha[g // HALF_GROUPS][:, column : column + 1]
+                if k in SCALAR_SCALED:
+                    nc.scalar.activation(out=e_o(k, j), in_=e_o(k, j), func=ACT.Copy, scale=factor)
+                else:
+                    nc.vector.tensor_scalar(out=e_o(k, j), in0=e_o(k, j), scalar1=factor, scalar2=None, op0=ALU.mult)
 
-        def blend_reciprocal(s):
-            beta[s] = three.tile([P, GROUP_TILES], F32, name="beta")
-            nc.vector.reciprocal(out=beta[s][:], in_=e_sum[s][:])
+        def blend_reciprocal(k):
+            n = width(k) // P
+            beta[k] = three.tile([P, GROUP_TILES], F32, name="beta")
+            nc.vector.reciprocal(out=beta[k][:, :n], in_=e_sum[k][:, :n])
 
-        def blend_beta(s):
-            g = s - GROUPS
-            member = g % HALF_GROUPS
+        def blend_beta(k):
+            g, first, last = PIECES[k]
+            g -= GROUPS
+            column = (g % HALF_GROUPS) * GROUP_TILES
             nc.vector.scalar_tensor_tensor(
-                out=beta[s][:],
-                in0=beta[s][:],
+                out=beta[k][:, : last - first],
+                in0=beta[k][:, : last - first],
                 scalar=-1.0,
-                in1=minus_cond[g // HALF_GROUPS][:, member * GROUP_TILES : (member + 1) * GROUP_TILES],
+                in1=minus_cond[g // HALF_GROUPS][:, column + first : column + last],
                 op0=ALU.mult,
                 op1=ALU.mult,
             )
 
-        def blend_and_store(s):
-            g = s - GROUPS
-            for j in range(GROUP_TILES):
+        def blend_and_store(k):
+            g, first, last = PIECES[k]
+            for j in range(last - first):
                 nc.vector.scalar_tensor_tensor(
-                    out=e[s][:, j, :],
-                    in0=e[s][:, j, :],
-                    scalar=beta[s][:, j : j + 1],
-                    in1=e[g][:, j, :],
+                    out=e[k][:, j, :],
+                    in0=e[k][:, j, :],
+                    scalar=beta[k][:, j : j + 1],
+                    in1=e_o(k, j),
                     op0=ALU.mult,
                     op1=ALU.add,
                 )
-            nc.sync.dma_start(out=out_rows[:, g * GROUP_TILES : (g + 1) * GROUP_TILES, :], in_=e[s][:])
+            tiles = slice((g - GROUPS) * GROUP_TILES + first, (g - GROUPS) * GROUP_TILES + last)
+            nc.sync.dma_start(out=out_rows[:, tiles, :], in_=e[k][:, : last - first, :])
 
         load_x(0)
         nets.append(load_network(nc, keep, "o", W1o, b1o, W2o, b2o))
+        load_x(1)
         nc.sync.dma_start(out=b2_first_row[0:1, 0:CLASSES], in_=b2o.rearrange("(o c) -> o c", o=1))
         nc.sync.dma_start(out=b2_first_row[0:1, CLASSES:], in_=b2f.rearrange("(o c) -> o c", o=1))
-        load_x(1)
         load_x(2)
         nets.append(load_network(nc, keep, "f", W1f, b1f, W2f, b2f))
-        lay_out_w1(nc, "vector", nets[0], 0, PACK)
 
-        for i in range(-5, STEPS + 4):
-            run(load_x, i + 5, 3, GROUPS)
-            run(regroup_h, i, 0, STEPS)
+        for i in range(-5, COUNT + 4):
+            run(load_x, i + 5, 3, O_COUNT)
+            run(regroup_h, i, 0, COUNT)
             gate_slot()
-            run(quantise_x, i + 2, 0, GROUPS)
-            run(hidden_layer, i + 1, -1, STEPS + 2)
-            if i + 3 not in VECTOR_X_GROUPS:
-                run(lambda g: copy_x_out(g, 0), i + 3, 0, GROUPS)
-                run(lambda g: copy_x_out(g, 1), i + 3, 0, GROUPS)
+            if i == -3:
+                lay_out_w1(nc, "vector", nets[0], 0, PACK // 2)
+                lay_out_w1(nc, "vector", nets[0], PACK // 2, PACK)
+                quantise_w1(nc, nets[0], 0, PACK // 2)
+            run(quantise_x, i + 2, 0, O_COUNT)
+            if i == -2:
+                quantise_w1(nc, nets[0], PACK // 2, PACK)
+            run(hidden_layer, i + 1, -1, COUNT + 2)
+            if i + 3 not in VECTOR_X_PIECES:
+                run(copy_x_out, i + 3, 0, O_COUNT)
             if i == -3:
                 lay_out_rest(nc, "scalar", nets[0])
-                quantise_w1(nc, nets[0])
             if i == -1:
                 quantise_w2(nc, nets[0])
-            run(lambda s: statistics(s, "e1"), i - 3, 0, GROUPS)
-            run(blend_reciprocal, i - 3, GROUPS, STEPS)
-            if i + 2 >= GROUPS:
-                run(add_bias, i - 1, 0, GROUPS)
-                run(blend_scale_o, i - 2, GROUPS, STEPS)
+            run(lambda k: statistics(k, "e1"), i - 3, 0, O_COUNT)
+            run(blend_reciprocal, i - 3, O_COUNT, COUNT)
+            if i + 2 >= O_COUNT:
+                run(add_bias, i - 1, 0, COUNT)
+                if i - 2 not in SCALAR_SCALED:
+                    run(blend_scale_o, i - 2, O_COUNT, COUNT)
                 gate_slot()
-            run(quantise_h, i, 0, STEPS)
+            run(quantise_h, i, 0, COUNT)
             gate_slot()
-            run(head, i, 0, STEPS)
-            if i + 3 in VECTOR_X_GROUPS:
-                copy_x_out(i + 3, 0)
-                copy_x_out(i + 3, 1)
-            run(transpose_x, i + 4, 0, GROUPS)
-            if i + 2 < GROUPS:
-                run(add_bias, i - 1, 0, STEPS)
+            run(head, i, 0, COUNT)
+            if i + 3 in VECTOR_X_PIECES:
+                copy_x_out(i + 3)
+            run(transpose_x, i + 4, 0, O_COUNT)
+            if i + 2 < O_COUNT:
+                run(add_bias, i - 1, 0, COUNT)
                 gate_slot()
-            run(lambda s: statistics(s, "e4"), i - 3, 0, GROUPS)
-            run(blend_beta, i - 3, GROUPS, STEPS)
-            run(row_max, i - 1, 0, STEPS)
+            run(lambda k: statistics(k, "e4"), i - 3, 0, O_COUNT)
+            run(blend_beta, i - 3, O_COUNT, COUNT)
+            run(row_max, i - 1, 0, COUNT)
             gate_slot()
-            run(exponentials, i - 2, 0, STEPS)
-            run(blend_and_store, i - 3, GROUPS, STEPS)
-            if i == -1 or i == 0:
-                lay_out_w1(nc, "scalar", nets[1], 2 * (i + 1), 2 * (i + 2))
+            run(exponentials, i - 2, 0, COUNT)
+            if i - 2 in SCALAR_SCALED:
+                blend_scale_o(i - 2)
+            run(blend_and_store, i - 3, O_COUNT, COUNT)
+            if i == 0 or i == 1:
+                lay_out_w1(nc, "scalar", nets[1], 2 * i, 2 * (i + 1))
             if i == -2:
                 b2_spread = psum_l.tile([P, GROUP_TILES, CLASSES], F32, name="acc")
-                nc.tensor.matmul(out=b2_spread[:, 0, :], lhsT=ones[:], rhs=b2_first_row[:, 0:CLASSES], start=True, stop=True)
-                nc.tensor.matmul(out=b2_spread[:, 1, :], lhsT=b2_first_row[:, CLASSES:], rhs=ones[:], start=True, stop=True)
+                for n in range(2):
+                    row = b2_first_row[:, n * CLASSES : (n + 1) * CLASSES]
+                    nc.tensor.matmul(out=b2_spread[:, n, :], lhsT=ones[:], rhs=row, start=True, stop=True)
+                    nc.tensor.matmul(out=b2_spread[:, 2 + n, :], lhsT=row, rhs=ones[:], start=True, stop=True)
             if i == -1:
-                copy_on(nc, "scalar", nets[0]["b2"][:], b2_spread[:, 0, :])
-                copy_on(nc, "scalar", nets[1]["b2"][:], b2_spread[:, 1, 0:1])
-            if i == 1:
+                for n in range(2):
+                    copy_on(nc, "scalar", nets[n]["b2_row"][:], b2_spread[:, n, :])
+                copy_on(nc, "scalar", nets[1]["b2_col"][:], b2_spread[:, 3, 0:1])
+            if i == 2:
                 lay_out_rest(nc, "scalar", nets[1])
-            if i == 3:
-                quantise_w1(nc, nets[1])
+            if i == 4:
+                quantise_w1(nc, nets[1], 0, PACK)
                 quantise_w2(nc, nets[1])
-            if i - 3 in (HALF_GROUPS - 1, GROUPS - 1):
+            if i - 3 in (HALF_GROUPS, O_COUNT - 1):
                 assert issued[0] == len(waiting)
-                gate_half((i - 3) // HALF_GROUPS)
+                gate_half((i - 3) // HALF_GROUPS - 1)

@@ -35,7 +35,10 @@ SCALAR_SCALED = range(COUNT - 3, COUNT)
 WORDS = D_IN // 2
 TAU = 0.5
 SERIES_STEPS = 3
-VECTOR_X_PIECES = (3, 4)
+GPSIMD_PIECES = range(3, O_COUNT)
+GPSIMD_FROM = GROUP_ROWS // 2
+OVERLAP = 8
+VECTOR_X_BANKS = [(3, 0), (3, 1)] + [(k, 0) for k in range(5, O_COUNT, 2)]
 
 FLOPS = 2 * (2 * ROWS * D_IN * D_H + 2 * ROWS * D_H * CLASSES)
 
@@ -254,13 +257,16 @@ def tile_combnethe_pa_t_kernel(tc, x, W1o, b1o, W2o, b2o, W1f, b1f, W2f, b2f, ou
                         nc.tensor.transpose(bank[:, jj, u, :], x_words[:, start + u : start + WORDS : 2], identity[:])
                 x_t[k].append(bank)
 
-        def copy_x_out(k):
-            x_grouped[k] = two.tile([P, GROUP_ROWS * PACK], BF16, name="x_grouped", align_bytes=64)
+        def copy_x_out(k, on_vector):
+            if k not in x_grouped:
+                x_grouped[k] = two.tile([P, GROUP_ROWS * PACK], BF16, name="x_grouped", align_bytes=64)
             grouped_words = x_grouped[k][:].bitcast(F32)
             for pair, bank in enumerate(x_t[k]):
+                if ((k, pair) in VECTOR_X_BANKS) != on_vector:
+                    continue
                 out = grouped_words[:, pair * 2 * WORDS : (pair + 1) * 2 * WORDS].rearrange("p (j r u) -> p j r u", j=2, u=2)
                 in_ = bank[:].rearrange("p j u r -> p j r u")
-                if k in VECTOR_X_PIECES:
+                if on_vector:
                     nc.vector.tensor_copy(out=out, in_=in_)
                 else:
                     nc.scalar.copy(out=out, in_=in_)
@@ -289,7 +295,7 @@ def tile_combnethe_pa_t_kernel(tc, x, W1o, b1o, W2o, b2o, W1f, b1f, W2f, b2f, ou
 
         def hidden_layer(k):
             if 0 <= k < COUNT:
-                planes[k] = two.tile([P, PACK, GROUP_ROWS], BF16, name="planes")
+                planes[k] = three.tile([P, PACK, GROUP_ROWS], BF16, name="planes")
             for t in range(PACK):
                 if t == PACK // 2 and k - 2 in TURNED:
                     turn_logits(k - 2)
@@ -305,10 +311,21 @@ def tile_combnethe_pa_t_kernel(tc, x, W1o, b1o, W2o, b2o, W1f, b1f, W2f, b2f, ou
 
         def regroup_h(k):
             h_grouped[k] = two.tile([P, GROUP_ROWS, PACK], BF16, name="h_grouped", align_bytes=64)
+            rows = slice(0, GPSIMD_FROM + OVERLAP if k in GPSIMD_PIECES else width(k))
             nc.vector.tensor_copy(
-                out=h_grouped[k][:, : width(k), :].rearrange("p (c i) t -> p c t i", i=4),
-                in_=planes[k][:, :, : width(k)].rearrange("p t (c i) -> p c t i", i=4),
+                out=h_grouped[k][:, rows, :].rearrange("p (c i) t -> p c t i", i=4),
+                in_=planes[k][:, :, rows].rearrange("p t (c i) -> p c t i", i=4),
             )
+            if k in GPSIMD_PIECES:
+                rows = slice(GPSIMD_FROM, GROUP_ROWS)
+                nc.gpsimd.tensor_scalar(
+                    out=h_grouped[k][:, rows, :],
+                    in0=planes[k][:, :, rows].rearrange("p t r -> p r t"),
+                    scalar1=1.0,
+                    scalar2=0.0,
+                    op0=ALU.mult,
+                    op1=ALU.add,
+                )
 
         def quantise_h(k):
             h_q[k] = (
@@ -466,7 +483,9 @@ def tile_combnethe_pa_t_kernel(tc, x, W1o, b1o, W2o, b2o, W1f, b1f, W2f, b2f, ou
 
         for i in range(-5, COUNT + 4):
             run(load_x, i + 5, 3, O_COUNT)
-            run(regroup_h, i, 0, COUNT)
+            early = i < O_COUNT
+            if not early:
+                run(regroup_h, i, 0, COUNT)
             gate_slot()
             if i == -3:
                 lay_out_w1(nc, "vector", nets[0], 0, PACK // 2)
@@ -475,39 +494,42 @@ def tile_combnethe_pa_t_kernel(tc, x, W1o, b1o, W2o, b2o, W1f, b1f, W2f, b2f, ou
             run(quantise_x, i + 2, 0, O_COUNT)
             if i == -2:
                 quantise_w1(nc, nets[0], PACK // 2, PACK)
+            if early:
+                gate_slot()
+                run(regroup_h, i, 0, COUNT)
+                run(add_bias, i - 1, 0, COUNT)
             run(hidden_layer, i + 1, -1, COUNT + 2)
-            if i + 3 not in VECTOR_X_PIECES:
-                run(copy_x_out, i + 3, 0, O_COUNT)
+            run(lambda k: copy_x_out(k, False), i + 3, 0, O_COUNT)
+            run(lambda k: copy_x_out(k, True), i + 3, 0, O_COUNT)
             if i == -3:
                 lay_out_rest(nc, "scalar", nets[0])
             if i == -1:
                 quantise_w2(nc, nets[0])
             run(lambda k: statistics(k, "e1"), i - 3, 0, O_COUNT)
+            if early:
+                run(lambda k: statistics(k, "e4"), i - 3, 0, O_COUNT)
+                run(row_max, i - 1, 0, COUNT)
             run(blend_reciprocal, i - 3, O_COUNT, COUNT)
-            if i + 2 >= O_COUNT:
+            if not early:
                 run(add_bias, i - 1, 0, COUNT)
                 if i - 2 not in SCALAR_SCALED:
                     run(blend_scale_o, i - 2, O_COUNT, COUNT)
-                gate_slot()
+            gate_slot()
             run(quantise_h, i, 0, COUNT)
             gate_slot()
             run(head, i, 0, COUNT)
-            if i + 3 in VECTOR_X_PIECES:
-                copy_x_out(i + 3)
             run(transpose_x, i + 4, 0, O_COUNT)
-            if i + 2 < O_COUNT:
-                run(add_bias, i - 1, 0, COUNT)
+            if not early:
+                run(lambda k: statistics(k, "e4"), i - 3, 0, O_COUNT)
+                run(blend_beta, i - 3, O_COUNT, COUNT)
+                run(row_max, i - 1, 0, COUNT)
                 gate_slot()
-            run(lambda k: statistics(k, "e4"), i - 3, 0, O_COUNT)
-            run(blend_beta, i - 3, O_COUNT, COUNT)
-            run(row_max, i - 1, 0, COUNT)
-            gate_slot()
             run(exponentials, i - 2, 0, COUNT)
             if i - 2 in SCALAR_SCALED:
                 blend_scale_o(i - 2)
             run(blend_and_store, i - 3, O_COUNT, COUNT)
-            if i == 0 or i == 1:
-                lay_out_w1(nc, "scalar", nets[1], 2 * i, 2 * (i + 1))
+            if i == 1 or i == 2:
+                lay_out_w1(nc, "vector", nets[1], 2 * (i - 1), 2 * (i - 1 + 1))
             if i == -2:
                 b2_spread = psum_l.tile([P, GROUP_TILES, CLASSES], F32, name="acc")
                 for n in range(2):

@@ -36,9 +36,9 @@ WORDS = D_IN // 2
 TAU = 0.5
 SERIES_STEPS = 3
 GPSIMD_PIECES = range(3, O_COUNT)
-GPSIMD_FROM = GROUP_ROWS // 2
+GPSIMD_FROM = 3 * GROUP_ROWS // 8
 OVERLAP = 8
-VECTOR_X_BANKS = [(3, 0), (3, 1)] + [(k, 0) for k in range(5, O_COUNT, 2)]
+VECTOR_X_BANKS = [(2, 0), (2, 1), (3, 0)] + [(k, 0) for k in range(4, O_COUNT - 1, 2)]
 
 FLOPS = 2 * (2 * ROWS * D_IN * D_H + 2 * ROWS * D_H * CLASSES)
 
@@ -497,6 +497,7 @@ def tile_combnethe_pa_t_kernel(tc, x, W1o, b1o, W2o, b2o, W1f, b1f, W2f, b2f, ou
             if early:
                 gate_slot()
                 run(regroup_h, i, 0, COUNT)
+                run(lambda k: statistics(k, "e1"), i - 3, 0, O_COUNT)
                 run(add_bias, i - 1, 0, COUNT)
             run(hidden_layer, i + 1, -1, COUNT + 2)
             run(lambda k: copy_x_out(k, False), i + 3, 0, O_COUNT)
@@ -505,7 +506,8 @@ def tile_combnethe_pa_t_kernel(tc, x, W1o, b1o, W2o, b2o, W1f, b1f, W2f, b2f, ou
                 lay_out_rest(nc, "scalar", nets[0])
             if i == -1:
                 quantise_w2(nc, nets[0])
-            run(lambda k: statistics(k, "e1"), i - 3, 0, O_COUNT)
+            if not early:
+                run(lambda k: statistics(k, "e1"), i - 3, 0, O_COUNT)
             if early:
                 run(lambda k: statistics(k, "e4"), i - 3, 0, O_COUNT)
                 run(row_max, i - 1, 0, COUNT)
@@ -517,8 +519,8 @@ def tile_combnethe_pa_t_kernel(tc, x, W1o, b1o, W2o, b2o, W1f, b1f, W2f, b2f, ou
             gate_slot()
             run(quantise_h, i, 0, COUNT)
             gate_slot()
-            run(head, i, 0, COUNT)
             run(transpose_x, i + 4, 0, O_COUNT)
+            run(head, i, 0, COUNT)
             if not early:
                 run(lambda k: statistics(k, "e4"), i - 3, 0, O_COUNT)
                 run(blend_beta, i - 3, O_COUNT, COUNT)

@@ -30,9 +30,11 @@ PIECES = (
 )
 COUNT = len(PIECES)
 O_COUNT = GROUPS + 1
-TURNED = range(O_COUNT, COUNT - 2)
-SCALAR_SCALED = range(COUNT - 3, COUNT)
+TURNED = range(O_COUNT, COUNT - 1)
+SECOND = range(O_COUNT + 1, COUNT - 9, 2)
+SCALAR_SCALED = range(COUNT - 5, COUNT)
 WORDS = D_IN // 2
+WARM_UPS = 6
 TAU = 0.5
 SERIES_STEPS = 3
 GPSIMD_PIECES = range(3, O_COUNT)
@@ -66,17 +68,11 @@ def copy_on(nc, engine, out, in_):
         nc.scalar.copy(out=out, in_=in_)
 
 
-def load_network(nc, keep, net, w1, b1, w2, b2):
-    w1_raw = keep.tile([P, PACK, D_H], BF16, name="w1_raw_" + net)
-    nc.sync.dma_start(out=w1_raw[:], in_=w1.rearrange("(p j) h -> p j h", j=PACK))
-    b1_raw = keep.tile([P, PACK], BF16, name="b1_raw_" + net)
-    nc.sync.dma_start(out=b1_raw[:], in_=b1.rearrange("(p t) -> p t", t=PACK))
-    w2_raw = keep.tile([P, PACK, CLASSES], BF16, name="w2_raw_" + net)
-    nc.sync.dma_start(out=w2_raw[:], in_=w2.rearrange("(p t) c -> p t c", t=PACK))
+def network_tiles(keep, net):
     return {
-        "w1_raw": w1_raw,
-        "b1_raw": b1_raw,
-        "w2_raw": w2_raw,
+        "w1_raw": keep.tile([P, PACK, D_H], BF16, name="w1_raw_" + net),
+        "b1_raw": keep.tile([P, PACK], BF16, name="b1_raw_" + net),
+        "w2_raw": keep.tile([P, PACK, CLASSES], BF16, name="w2_raw_" + net),
         "w1_grouped": keep.tile([P, D_H, PACK], BF16, name="w1_grouped_" + net, align_bytes=64),
         "w2_grouped": keep.tile([P, CLASSES, PACK], BF16, name="w2_grouped_" + net, align_bytes=64),
         "w1": (
@@ -93,18 +89,33 @@ def load_network(nc, keep, net, w1, b1, w2, b2):
     }
 
 
-def lay_out_w1(nc, engine, net, first, last):
+def load_first(nc, net, w1, b1):
+    nc.sync.dma_start(out=net["b1_raw"][:], in_=b1.rearrange("(p t) -> p t", t=PACK))
+    for first in range(0, D_H, D_H // 2):
+        cols = slice(first, first + D_H // 2)
+        nc.sync.dma_start(out=net["w1_raw"][:, :, cols], in_=w1.rearrange("(p j) h -> p j h", j=PACK)[:, :, cols])
+
+
+def load_w2(nc, net, w2):
+    nc.sync.dma_start(out=net["w2_raw"][:], in_=w2.rearrange("(p t) c -> p t c", t=PACK))
+
+
+def lay_out_w1(nc, net, half):
+    units = slice(half * P // 2, (half + 1) * P // 2)
     copy_on(
         nc,
-        engine,
-        net["w1_grouped"][:].rearrange("p (t m) j -> p t m j", t=PACK)[:, first:last],
-        net["w1_raw"][:].rearrange("p j (m t) -> p t m j", t=PACK)[:, first:last],
+        "vector",
+        net["w1_grouped"][:].rearrange("p (t m) j -> p t m j", t=PACK)[:, :, units],
+        net["w1_raw"][:].rearrange("p j (m t) -> p t m j", t=PACK)[:, :, units],
     )
 
 
-def lay_out_rest(nc, engine, net):
-    copy_on(nc, engine, net["b1"][:], net["b1_raw"][:])
-    copy_on(nc, engine, net["w2_grouped"][:], net["w2_raw"][:].rearrange("p t c -> p c t"))
+def lay_out_b1(nc, net):
+    copy_on(nc, "scalar", net["b1"][:], net["b1_raw"][:])
+
+
+def lay_out_w2(nc, net):
+    copy_on(nc, "scalar", net["w2_grouped"][:], net["w2_raw"][:].rearrange("p t c -> p c t"))
 
 
 def quantise_w1(nc, net, first, last):
@@ -157,11 +168,10 @@ def gate_slots(nc, gate, stats, half):
     mean4, spread4 = stats["e4"][:, cols, 1], stats["e4"][:, cols, 2]
     n = float(CLASSES)
     r1, r2, r4, r8 = new("r1"), new("r2"), new("r4"), new("r8")
-    recip1 = new("recip1")
     part0, part1, part2 = new("part0"), new("part1"), new("part2")
     part1_squared = new("part1_squared")
     slots.append([lambda: nc.vector.reciprocal(out=r1[:], in_=mean1)])
-    slots.append([mul(r2, r1[:], r1[:]), affine(recip1, r1, 1.0 / n, 0.0)])
+    slots.append([mul(r2, r1[:], r1[:])])
     slots.append([mul(part0, spread1, r2[:]), mul(r4, r2[:], r2[:])])
 
     a0 = series(
@@ -185,8 +195,8 @@ def gate_slots(nc, gate, stats, half):
     a2 = series(rest2, -(c0**4) / n**8, 1.0, "2", [])
 
     minus_cond, alpha = new("minus_cond"), new("alpha")
-    slots.append([fused(minus_cond, square1, -(TAU**8) * c0**4, ALU.mult, a2)])
-    slots.append([fused(alpha, minus_cond, 1.0, ALU.add, recip1)])
+    slots.append([fused(minus_cond, square1, -(TAU**8) * c0**4 / n, ALU.mult, a2)])
+    slots.append([fused(alpha, minus_cond, 1.0 / n, ALU.add, r1)])
     return slots, minus_cond, alpha
 
 
@@ -201,15 +211,20 @@ def tile_combnethe_pa_t_kernel(tc, x, W1o, b1o, W2o, b2o, W1f, b1f, W2f, b2f, ou
         gate = pools.enter_context(tc.tile_pool(name="gate", bufs=1))
         two = pools.enter_context(tc.tile_pool(name="two", bufs=2))
         three = pools.enter_context(tc.tile_pool(name="three", bufs=3))
-        five = pools.enter_context(tc.tile_pool(name="five", bufs=5))
+        four = pools.enter_context(tc.tile_pool(name="four", bufs=4))
+        six = pools.enter_context(tc.tile_pool(name="six", bufs=6))
         psum_x = pools.enter_context(tc.psum_pool(name="psum_x", bufs=2))
         psum_z = pools.enter_context(tc.psum_pool(name="psum_z", bufs=4))
         psum_l = pools.enter_context(tc.psum_pool(name="psum_l", bufs=2))
 
-        identity = keep.tile([P, P], F32, name="identity")
-        make_identity(nc, identity[:])
         ones = keep.tile([P, P], BF16, name="ones")
         nc.gpsimd.memset(ones[:], 1.0)
+        for warm_up in range(WARM_UPS):
+            bank = psum_z.tile([P, GROUP_ROWS], F32, name="z")
+            moving = ones[:].unsqueeze(1).to_broadcast([P, GROUP_TILES, P])
+            nc.tensor.matmul(out=bank[:].rearrange("p (j r) -> p j r", j=GROUP_TILES), lhsT=ones[:], rhs=moving, start=True, stop=True)
+        identity = keep.tile([P, P], F32, name="identity")
+        make_identity(nc, identity[:])
         b2_first_row = keep.tile([P, 2 * CLASSES], BF16, name="b2_first_row")
         nc.gpsimd.memset(b2_first_row[:], 0.0)
         warm = keep.tile([P, 1], F32, name="warm")
@@ -339,7 +354,9 @@ def tile_combnethe_pa_t_kernel(tc, x, W1o, b1o, W2o, b2o, W1f, b1f, W2f, b2f, ou
             w2 = net_of(k)["w2"]
             acc[k] = psum_l.tile([P, GROUP_TILES, CLASSES], F32, name="acc")
             if k in TURNED:
-                mx_pass(nc, acc[k][:].rearrange("p j r -> p (j r)"), (w2[0][:], w2[1][:]), (h_q[k][0][:], h_q[k][1][:]))
+                n = width(k)
+                out = acc[k][:].rearrange("p j r -> p (j r)")[:, :n]
+                mx_pass(nc, out, (w2[0][:], w2[1][:]), (h_q[k][0][:, :n], h_q[k][1][:, :n]))
             else:
                 for j in range(width(k) // P):
                     cols = slice(j * P, (j + 1) * P)
@@ -359,11 +376,16 @@ def tile_combnethe_pa_t_kernel(tc, x, W1o, b1o, W2o, b2o, W1f, b1f, W2f, b2f, ou
 
         def turn_logits(k):
             class_rows = two.tile([P, GROUP_TILES, P], F32, name="class_rows")
+            n = width(k) // P
             nc.scalar.activation(
-                out=class_rows[:], in_=acc[k][:], func=ACT.Identity, bias=net_of(k)["b2_col"][:, 0:1], scale=1.0
+                out=class_rows[:, :n, :],
+                in_=acc[k][:, :n, :],
+                func=ACT.Identity,
+                bias=net_of(k)["b2_col"][:, 0:1],
+                scale=1.0,
             )
             logits[k] = psum_x.tile([P, GROUP_TILES, CLASSES], F32, name="x_t")
-            for j in range(GROUP_TILES):
+            for j in range(n):
                 nc.tensor.transpose(logits[k][:, j, :], class_rows[:, j, :], identity[:])
 
         def row_max(k):
@@ -389,8 +411,10 @@ def tile_combnethe_pa_t_kernel(tc, x, W1o, b1o, W2o, b2o, W1f, b1f, W2f, b2f, ou
                         out=e4[k][:, j, :], in_=logits[k][:, j, :], func=ACT.Exp, bias=neg_max4[:, j : j + 1], scale=4.0
                     )
             else:
-                e[k] = five.tile([P, GROUP_TILES, CLASSES], F32, name="e_f")
-                e_sum[k] = three.tile([P, GROUP_TILES], F32, name="sum_f")
+                e[k] = six.tile([P, GROUP_TILES, CLASSES], F32, name="e_f")
+                if k not in SECOND:
+                    e_sum[k] = four.tile([P, 2 * GROUP_TILES], F32, name="sum_f")
+                sums = e_sum[k - 1][:, GROUP_TILES:] if k in SECOND else e_sum[k][:]
                 for j in range(n):
                     nc.scalar.activation(
                         out=e[k][:, j, :],
@@ -398,8 +422,11 @@ def tile_combnethe_pa_t_kernel(tc, x, W1o, b1o, W2o, b2o, W1f, b1f, W2f, b2f, ou
                         func=ACT.Exp,
                         bias=neg_max[k][:, j : j + 1],
                         scale=1.0,
-                        accum_out=e_sum[k][:, j : j + 1],
+                        accum_out=sums[:, j : j + 1],
                     )
+
+        def sums_f(k):
+            return e_sum[k], 2 * GROUP_TILES if k + 1 in SECOND else width(k) // P
 
         def statistics(k, power):
             g, first, last = PIECES[k]
@@ -423,6 +450,10 @@ def tile_combnethe_pa_t_kernel(tc, x, W1o, b1o, W2o, b2o, W1f, b1f, W2f, b2f, ou
                     instruction()
                 issued[0] += 1
 
+        def pieces_to_blend(turn):
+            paired = range(O_COUNT, SECOND[-1] + 1)
+            return [k for k in range(O_COUNT, COUNT) if turn == k + (4 if k in paired else 3)]
+
         def e_o(k, j):
             g, tile = PIECES[k][0] - GROUPS, PIECES[k][1] + j
             for other, (step, first, last) in enumerate(PIECES[:O_COUNT]):
@@ -442,30 +473,36 @@ def tile_combnethe_pa_t_kernel(tc, x, W1o, b1o, W2o, b2o, W1f, b1f, W2f, b2f, ou
                     nc.vector.tensor_scalar(out=e_o(k, j), in0=e_o(k, j), scalar1=factor, scalar2=None, op0=ALU.mult)
 
         def blend_reciprocal(k):
-            n = width(k) // P
-            beta[k] = three.tile([P, GROUP_TILES], F32, name="beta")
-            nc.vector.reciprocal(out=beta[k][:, :n], in_=e_sum[k][:, :n])
+            tile, columns = sums_f(k)
+            reciprocal = four.tile([P, 2 * GROUP_TILES], F32, name="reciprocal")
+            nc.vector.reciprocal(out=reciprocal[:, :columns], in_=tile[:, :columns])
+            beta[k] = (reciprocal, columns)
 
         def blend_beta(k):
             g, first, last = PIECES[k]
             g -= GROUPS
-            column = (g % HALF_GROUPS) * GROUP_TILES
+            tile, columns = beta[k]
+            column = (g % HALF_GROUPS) * GROUP_TILES + first
             nc.vector.scalar_tensor_tensor(
-                out=beta[k][:, : last - first],
-                in0=beta[k][:, : last - first],
-                scalar=-1.0,
-                in1=minus_cond[g // HALF_GROUPS][:, column + first : column + last],
+                out=tile[:, :columns],
+                in0=tile[:, :columns],
+                scalar=-float(CLASSES),
+                in1=minus_cond[g // HALF_GROUPS][:, column : column + columns],
                 op0=ALU.mult,
                 op1=ALU.mult,
             )
 
         def blend_and_store(k):
             g, first, last = PIECES[k]
+            if k in SECOND:
+                factor = beta[k - 1][0][:, GROUP_TILES:]
+            else:
+                factor = beta[k][0][:]
             for j in range(last - first):
                 nc.vector.scalar_tensor_tensor(
                     out=e[k][:, j, :],
                     in0=e[k][:, j, :],
-                    scalar=beta[k][:, j : j + 1],
+                    scalar=factor[:, j : j + 1],
                     in1=e_o(k, j),
                     op0=ALU.mult,
                     op1=ALU.add,
@@ -473,13 +510,16 @@ def tile_combnethe_pa_t_kernel(tc, x, W1o, b1o, W2o, b2o, W1f, b1f, W2f, b2f, ou
             tiles = slice((g - GROUPS) * GROUP_TILES + first, (g - GROUPS) * GROUP_TILES + last)
             nc.sync.dma_start(out=out_rows[:, tiles, :], in_=e[k][:, : last - first, :])
 
+        nets.extend([network_tiles(keep, "o"), network_tiles(keep, "f")])
         load_x(0)
-        nets.append(load_network(nc, keep, "o", W1o, b1o, W2o, b2o))
+        load_first(nc, nets[0], W1o, b1o)
         load_x(1)
+        load_w2(nc, nets[0], W2o)
         nc.sync.dma_start(out=b2_first_row[0:1, 0:CLASSES], in_=b2o.rearrange("(o c) -> o c", o=1))
         nc.sync.dma_start(out=b2_first_row[0:1, CLASSES:], in_=b2f.rearrange("(o c) -> o c", o=1))
         load_x(2)
-        nets.append(load_network(nc, keep, "f", W1f, b1f, W2f, b2f))
+        load_first(nc, nets[1], W1f, b1f)
+        load_w2(nc, nets[1], W2f)
 
         for i in range(-5, COUNT + 4):
             run(load_x, i + 5, 3, O_COUNT)
@@ -488,8 +528,8 @@ def tile_combnethe_pa_t_kernel(tc, x, W1o, b1o, W2o, b2o, W1f, b1f, W2f, b2f, ou
                 run(regroup_h, i, 0, COUNT)
             gate_slot()
             if i == -3:
-                lay_out_w1(nc, "vector", nets[0], 0, PACK // 2)
-                lay_out_w1(nc, "vector", nets[0], PACK // 2, PACK)
+                lay_out_w1(nc, nets[0], 0)
+                lay_out_w1(nc, nets[0], 1)
                 quantise_w1(nc, nets[0], 0, PACK // 2)
             run(quantise_x, i + 2, 0, O_COUNT)
             if i == -2:
@@ -503,15 +543,20 @@ def tile_combnethe_pa_t_kernel(tc, x, W1o, b1o, W2o, b2o, W1f, b1f, W2f, b2f, ou
             run(lambda k: copy_x_out(k, False), i + 3, 0, O_COUNT)
             run(lambda k: copy_x_out(k, True), i + 3, 0, O_COUNT)
             if i == -3:
-                lay_out_rest(nc, "scalar", nets[0])
+                lay_out_b1(nc, nets[0])
             if i == -1:
+                lay_out_w2(nc, nets[0])
+            if i == 0:
                 quantise_w2(nc, nets[0])
             if not early:
                 run(lambda k: statistics(k, "e1"), i - 3, 0, O_COUNT)
             if early:
                 run(lambda k: statistics(k, "e4"), i - 3, 0, O_COUNT)
                 run(row_max, i - 1, 0, COUNT)
-            run(blend_reciprocal, i - 3, O_COUNT, COUNT)
+            due = pieces_to_blend(i)
+            for k in due:
+                if k not in SECOND:
+                    blend_reciprocal(k)
             if not early:
                 run(add_bias, i - 1, 0, COUNT)
                 if i - 2 not in SCALAR_SCALED:
@@ -523,15 +568,18 @@ def tile_combnethe_pa_t_kernel(tc, x, W1o, b1o, W2o, b2o, W1f, b1f, W2f, b2f, ou
             run(head, i, 0, COUNT)
             if not early:
                 run(lambda k: statistics(k, "e4"), i - 3, 0, O_COUNT)
-                run(blend_beta, i - 3, O_COUNT, COUNT)
+                for k in due:
+                    if k not in SECOND:
+                        blend_beta(k)
                 run(row_max, i - 1, 0, COUNT)
                 gate_slot()
+            if i - 3 in SCALAR_SCALED:
+                blend_scale_o(i - 3)
             run(exponentials, i - 2, 0, COUNT)
-            if i - 2 in SCALAR_SCALED:
-                blend_scale_o(i - 2)
-            run(blend_and_store, i - 3, O_COUNT, COUNT)
+            for k in due:
+                blend_and_store(k)
             if i == 1 or i == 2:
-                lay_out_w1(nc, "vector", nets[1], 2 * (i - 1), 2 * (i - 1 + 1))
+                lay_out_w1(nc, nets[1], i - 1)
             if i == -2:
                 b2_spread = psum_l.tile([P, GROUP_TILES, CLASSES], F32, name="acc")
                 for n in range(2):
@@ -543,7 +591,8 @@ def tile_combnethe_pa_t_kernel(tc, x, W1o, b1o, W2o, b2o, W1f, b1f, W2f, b2f, ou
                     copy_on(nc, "scalar", nets[n]["b2_row"][:], b2_spread[:, n, :])
                 copy_on(nc, "scalar", nets[1]["b2_col"][:], b2_spread[:, 3, 0:1])
             if i == 2:
-                lay_out_rest(nc, "scalar", nets[1])
+                lay_out_b1(nc, nets[1])
+                lay_out_w2(nc, nets[1])
             if i == 4:
                 quantise_w1(nc, nets[1], 0, PACK)
                 quantise_w2(nc, nets[1])

@@ -526,7 +526,7 @@ def tile_combnethe_pa_t_kernel(tc, x, W1o, b1o, W2o, b2o, W1f, b1f, W2f, b2f, ou
             early = i < O_COUNT
             if not early:
                 run(regroup_h, i, 0, COUNT)
-            gate_slot()
+                gate_slot()
             if i == -3:
                 lay_out_w1(nc, nets[0], 0)
                 lay_out_w1(nc, nets[0], 1)
@@ -535,8 +535,10 @@ def tile_combnethe_pa_t_kernel(tc, x, W1o, b1o, W2o, b2o, W1f, b1f, W2f, b2f, ou
             if i == -2:
                 quantise_w1(nc, nets[0], PACK // 2, PACK)
             if early:
-                gate_slot()
+                if i + 2 < O_COUNT:
+                    gate_slot()
                 run(regroup_h, i, 0, COUNT)
+                gate_slot()
                 run(lambda k: statistics(k, "e1"), i - 3, 0, O_COUNT)
                 run(add_bias, i - 1, 0, COUNT)
             run(hidden_layer, i + 1, -1, COUNT + 2)
@@ -564,8 +566,8 @@ def tile_combnethe_pa_t_kernel(tc, x, W1o, b1o, W2o, b2o, W1f, b1f, W2f, b2f, ou
             gate_slot()
             run(quantise_h, i, 0, COUNT)
             gate_slot()
-            run(transpose_x, i + 4, 0, O_COUNT)
             run(head, i, 0, COUNT)
+            run(transpose_x, i + 4, 0, O_COUNT)
             if not early:
                 run(lambda k: statistics(k, "e4"), i - 3, 0, O_COUNT)
                 for k in due:

@@ -40,7 +40,7 @@ SERIES_STEPS = 3
 GPSIMD_PIECES = range(3, O_COUNT)
 GPSIMD_FROM = 3 * GROUP_ROWS // 8
 OVERLAP = 8
-VECTOR_X_BANKS = [(2, 0), (2, 1), (3, 0)] + [(k, 0) for k in range(4, O_COUNT - 1, 2)]
+VECTOR_X_BANKS = [(2, 0), (2, 1), (3, 0)] + [(k, 0) for k in range(4, 13, 2)]
 
 FLOPS = 2 * (2 * ROWS * D_IN * D_H + 2 * ROWS * D_H * CLASSES)
 
@@ -236,6 +236,7 @@ def tile_combnethe_pa_t_kernel(tc, x, W1o, b1o, W2o, b2o, W1f, b1f, W2f, b2f, ou
         for power in ("e1", "e4"):
             stats[power] = gate.tile([P, TILES, 3], F32, name="stats_" + power)
         minus_cond, alpha = [], []
+        complete = []
         waiting, issued = [], [0]
         x_sb, x_t, x_grouped, x_q = {}, {}, {}, {}
         planes, z, h_grouped, h_q, acc, logits, neg_max, e, e4, e_sum, beta = {}, {}, {}, {}, {}, {}, {}, {}, {}, {}, {}
@@ -312,7 +313,7 @@ def tile_combnethe_pa_t_kernel(tc, x, W1o, b1o, W2o, b2o, W1f, b1f, W2f, b2f, ou
             if 0 <= k < COUNT:
                 planes[k] = three.tile([P, PACK, GROUP_ROWS], BF16, name="planes")
             for t in range(PACK):
-                if t == PACK // 2 and k - 2 in TURNED:
+                if t == 1 and k - 2 in TURNED:
                     turn_logits(k - 2)
                 if 0 <= k < COUNT:
                     nc.scalar.activation(
@@ -441,6 +442,7 @@ def tile_combnethe_pa_t_kernel(tc, x, W1o, b1o, W2o, b2o, W1f, b1f, W2f, b2f, ou
         def gate_half(half):
             slots, minus_cond_half, alpha_half = gate_slots(nc, gate, stats, half)
             waiting.extend(slots)
+            complete.append(len(waiting))
             minus_cond.append(minus_cond_half)
             alpha.append(alpha_half)
 
@@ -463,7 +465,7 @@ def tile_combnethe_pa_t_kernel(tc, x, W1o, b1o, W2o, b2o, W1f, b1f, W2f, b2f, ou
         def blend_scale_o(k):
             g, first, last = PIECES[k]
             g -= GROUPS
-            assert issued[0] == len(waiting) or g % HALF_GROUPS > 0
+            assert issued[0] >= complete[g // HALF_GROUPS]
             for j in range(last - first):
                 column = (g % HALF_GROUPS) * GROUP_TILES + first + j
                 factor = alpha[g // HALF_GROUPS][:, column : column + 1]
@@ -538,7 +540,6 @@ def tile_combnethe_pa_t_kernel(tc, x, W1o, b1o, W2o, b2o, W1f, b1f, W2f, b2f, ou
                 if i + 2 < O_COUNT:
                     gate_slot()
                 run(regroup_h, i, 0, COUNT)
-                gate_slot()
                 run(lambda k: statistics(k, "e1"), i - 3, 0, O_COUNT)
                 run(add_bias, i - 1, 0, COUNT)
             run(hidden_layer, i + 1, -1, COUNT + 2)
@@ -561,13 +562,13 @@ def tile_combnethe_pa_t_kernel(tc, x, W1o, b1o, W2o, b2o, W1f, b1f, W2f, b2f, ou
                     blend_reciprocal(k)
             if not early:
                 run(add_bias, i - 1, 0, COUNT)
-                if i - 2 not in SCALAR_SCALED:
-                    run(blend_scale_o, i - 2, O_COUNT, COUNT)
+                if i - 3 not in SCALAR_SCALED:
+                    run(blend_scale_o, i - 3, O_COUNT, COUNT)
             gate_slot()
             run(quantise_h, i, 0, COUNT)
             gate_slot()
-            run(head, i, 0, COUNT)
             run(transpose_x, i + 4, 0, O_COUNT)
+            run(head, i, 0, COUNT)
             if not early:
                 run(lambda k: statistics(k, "e4"), i - 3, 0, O_COUNT)
                 for k in due:

from contextlib import ExitStack

import concourse.mybir as mybir
from concourse.masks import make_identity

F32 = mybir.dt.float32
BF16 = mybir.dt.bfloat16
U32 = mybir.dt.uint32
U8 = mybir.dt.uint8
FP8X4 = mybir.dt.float8_e4m3fn_x4
ACT = mybir.ActivationFunctionType
ALU = mybir.AluOpType
AXIS = mybir.AxisListType

P = 128
PACK = 4
ROWS, D_IN, D_H, CLASSES = 8192, 512, 512, 128
TILES = ROWS // P
GROUP_TILES = 4
GROUP_ROWS = GROUP_TILES * P
GROUPS = TILES // GROUP_TILES
STEPS = 2 * GROUPS
HALF_GROUPS = GROUPS // 2
HALF_TILES = TILES // 2
HALVES = ((0, GROUP_TILES // 2), (GROUP_TILES // 2, GROUP_TILES))
PIECES = (
    [(0, first, last) for first, last in HALVES]
    + [(step, 0, GROUP_TILES) for step in range(1, STEPS - 1)]
    + [(STEPS - 1, first, last) for first, last in HALVES]
)
COUNT = len(PIECES)
O_COUNT = GROUPS + 1
TURNED = range(O_COUNT, COUNT - 1)
SECOND = range(O_COUNT + 1, COUNT - 9, 2)
SCALAR_SCALED = range(COUNT - 5, COUNT)
WORDS = D_IN // 2
WARM_UPS = 6
TAU = 0.5
SERIES_STEPS = 3
GPSIMD_PIECES = range(3, O_COUNT)
GPSIMD_FROM = 3 * GROUP_ROWS // 8
OVERLAP = 8
VECTOR_X_BANKS = [(2, 0), (2, 1), (3, 0)] + [(k, 0) for k in range(4, 13, 2)]

FLOPS = 2 * (2 * ROWS * D_IN * D_H + 2 * ROWS * D_H * CLASSES)


def quantise(nc, grouped, codes, scales):
    nc.vector.quantize_mx(out=codes.bitcast(FP8X4), scales=scales, in_=grouped)


def mx_pass(nc, acc, stationary, moving):
    nc.tensor.matmul_mx(
        out=acc,
        lhsT=stationary[0].bitcast(FP8X4),
        lhsT_scale=stationary[1],
        rhs=moving[0].bitcast(FP8X4),
        rhs_scale=moving[1],
        start=True,
        stop=True,
    )


def copy_on(nc, engine, out, in_):
    if engine == "vector":
        nc.vector.tensor_scalar(out=out, in0=in_, scalar1=1.0, scalar2=0.0, op0=ALU.mult, op1=ALU.add)
    else:
        nc.scalar.copy(out=out, in_=in_)


def network_tiles(keep, net):
    return {
        "w1_raw": keep.tile([P, PACK, D_H], BF16, name="w1_raw_" + net),
        "b1_raw": keep.tile([P, PACK], BF16, name="b1_raw_" + net),
        "w2_raw": keep.tile([P, PACK, CLASSES], BF16, name="w2_raw_" + net),
        "w1_grouped": keep.tile([P, D_H, PACK], BF16, name="w1_grouped_" + net, align_bytes=64),
        "w2_grouped": keep.tile([P, CLASSES, PACK], BF16, name="w2_grouped_" + net, align_bytes=64),
        "w1": (
            keep.tile([P, D_H], U32, name="w1_codes_" + net, align_bytes=64),
            keep.tile([P, D_H], U8, name="w1_scales_" + net, align_bytes=64),
        ),
        "w2": (
            keep.tile([P, CLASSES], U32, name="w2_codes_" + net, align_bytes=64),
            keep.tile([P, CLASSES], U8, name="w2_scales_" + net, align_bytes=64),
        ),
        "b1": keep.tile([P, PACK], F32, name="b1_cols_" + net),
        "b2_row": keep.tile([P, CLASSES], F32, name="b2_row_" + net),
        "b2_col": keep.tile([P, 1], F32, name="b2_col_" + net),
    }


def load_first(nc, net, w1, b1):
    nc.sync.dma_start(out=net["b1_raw"][:], in_=b1.rearrange("(p t) -> p t", t=PACK))
    for first in range(0, D_H, D_H // 2):
        cols = slice(first, first + D_H // 2)
        nc.sync.dma_start(out=net["w1_raw"][:, :, cols], in_=w1.rearrange("(p j) h -> p j h", j=PACK)[:, :, cols])


def load_w2(nc, net, w2):
    nc.sync.dma_start(out=net["w2_raw"][:], in_=w2.rearrange("(p t) c -> p t c", t=PACK))


def lay_out_w1(nc, net, half):
    units = slice(half * P // 2, (half + 1) * P // 2)
    copy_on(
        nc,
        "vector",
        net["w1_grouped"][:].rearrange("p (t m) j -> p t m j", t=PACK)[:, :, units],
        net["w1_raw"][:].rearrange("p j (m t) -> p t m j", t=PACK)[:, :, units],
    )


def lay_out_b1(nc, net):
    copy_on(nc, "scalar", net["b1"][:], net["b1_raw"][:])


def lay_out_w2(nc, net):
    copy_on(nc, "scalar", net["w2_grouped"][:], net["w2_raw"][:].rearrange("p t c -> p c t"))


def quantise_w1(nc, net, first, last):
    cols = slice(first * P, last * P)
    quantise(nc, net["w1_grouped"][:, cols, :].rearrange("p c j -> p (c j)"), net["w1"][0][:, cols], net["w1"][1][:, cols])


def quantise_w2(nc, net):
    quantise(nc, net["w2_grouped"][:].rearrange("p c t -> p (c t)"), net["w2"][0][:], net["w2"][1][:])


def gate_slots(nc, gate, stats, half):
    cols = slice(half * HALF_TILES, (half + 1) * HALF_TILES)
    tag = "_%d" % half
    slots = []

    def new(name):
        return gate.tile([P, HALF_TILES], F32, name=name + tag)

    def mul(out, in0, in1):
        return lambda: nc.vector.tensor_tensor(out=out[:], in0=in0, in1=in1, op=ALU.mult)

    def affine(out, in_, factor, shift):
        return lambda: nc.vector.tensor_scalar(
            out=out[:], in0=in_[:], scalar1=factor, scalar2=shift, op0=ALU.mult, op1=ALU.add
        )

    def fused(out, in0, scalar, op0, in1):
        return lambda: nc.vector.scalar_tensor_tensor(
            out=out[:], in0=in0[:], scalar=scalar, in1=in1[:], op0=op0, op1=ALU.mult
        )

    def plus(out, in0, factor, in1):
        return lambda: nc.vector.scalar_tensor_tensor(
            out=out[:], in0=in0[:], scalar=factor, in1=in1[:], op0=ALU.mult, op1=ALU.add
        )

    def series(total, factor, shift, name, fill):
        b = [new("b0_" + name), new("b1_" + name)]
        a = new("a_" + name)
        slots.append([affine(b[0], total, factor, shift)] + fill[:1])
        slots.append([affine(a, b[0], 1.0, 1.0), mul(b[1], b[0][:], b[0][:])])
        slots.append([mul(b[0], b[1][:], b[1][:]), fused(a, b[1], 1.0, ALU.add, a)])
        slots.append([mul(b[1], b[0][:], b[0][:]), fused(a, b[0], 1.0, ALU.add, a)])
        slots.append([fused(a, b[1], 1.0, ALU.add, a)] + fill[1:2])
        return a

    c0 = 2.0 / (2.0 + TAU**2)
    mean1, spread1 = stats["e1"][:, cols, 1], stats["e1"][:, cols, 2]
    mean4, spread4 = stats["e4"][:, cols, 1], stats["e4"][:, cols, 2]
    n = float(CLASSES)
    r1, r2, r4, r8 = new("r1"), new("r2"), new("r4"), new("r8")
    part0, part1, part2 = new("part0"), new("part1"), new("part2")
    part1_squared = new("part1_squared")
    slots.append([lambda: nc.vector.reciprocal(out=r1[:], in_=mean1)])
    slots.append([mul(r2, r1[:], r1[:])])
    slots.append([mul(part0, spread1, r2[:]), mul(r4, r2[:], r2[:])])

    a0 = series(
        part0,
        -c0 / n**2,
        1.0 - c0 * (TAU**2 + 1.0 / n),
        "0",
        [mul(part1, mean4, r4[:]), mul(r8, r4[:], r4[:])],
    )

    square0, rest1 = new("square0"), new("rest1")
    spread4_r8 = new("spread4_r8")
    slots.append([mul(square0, a0[:], a0[:]), mul(spread4_r8, spread4, r8[:])])
    slots.append([fused(rest1, part1, TAU**4 * n**3, ALU.add, square0), mul(part1_squared, part1[:], part1[:])])
    a1 = series(rest1, -(c0**2) / n**3, 1.0, "1", [plus(part2, part1_squared, n, spread4_r8)])

    both, square1, rest2 = new("both"), new("square1"), new("rest2")
    slots.append([mul(both, square0[:], a1[:])])
    slots.append([mul(square1, both[:], both[:])])
    slots.append([fused(rest2, part2, TAU**8 * n**8, ALU.add, square1)])
    a2 = series(rest2, -(c0**4) / n**8, 1.0, "2", [])

    minus_cond, alpha = new("minus_cond"), new("alpha")
    slots.append([fused(minus_cond, square1, -(TAU**8) * c0**4 / n, ALU.mult, a2)])
    slots.append([fused(alpha, minus_cond, 1.0 / n, ALU.add, r1)])
    return slots, minus_cond, alpha


def tile_combnethe_pa_t_kernel(tc, x, W1o, b1o, W2o, b2o, W1f, b1f, W2f, b2f, out):
    nc = tc.nc
    x_rows = x.rearrange("(p j) k -> p j k", j=TILES)
    out_rows = out.rearrange("(p j) c -> p j c", j=TILES)

    with ExitStack() as pools:
        pools.enter_context(tc.manual_schedule())
        keep = pools.enter_context(tc.tile_pool(name="keep", bufs=1))
        gate = pools.enter_context(tc.tile_pool(name="gate", bufs=1))
        two = pools.enter_context(tc.tile_pool(name="two", bufs=2))
        three = pools.enter_context(tc.tile_pool(name="three", bufs=3))
        four = pools.enter_context(tc.tile_pool(name="four", bufs=4))
        six = pools.enter_context(tc.tile_pool(name="six", bufs=6))
        psum_x = pools.enter_context(tc.psum_pool(name="psum_x", bufs=2))
        psum_z = pools.enter_context(tc.psum_pool(name="psum_z", bufs=4))
        psum_l = pools.enter_context(tc.psum_pool(name="psum_l", bufs=2))

        ones = keep.tile([P, P], BF16, name="ones")
        nc.gpsimd.memset(ones[:], 1.0)
        for warm_up in range(WARM_UPS):
            bank = psum_z.tile([P, GROUP_ROWS], F32, name="z")
            moving = ones[:].unsqueeze(1).to_broadcast([P, GROUP_TILES, P])
            nc.tensor.matmul(out=bank[:].rearrange("p (j r) -> p j r", j=GROUP_TILES), lhsT=ones[:], rhs=moving, start=True, stop=True)
        identity = keep.tile([P, P], F32, name="identity")
        make_identity(nc, identity[:])
        b2_first_row = keep.tile([P, 2 * CLASSES], BF16, name="b2_first_row")
        nc.gpsimd.memset(b2_first_row[:], 0.0)
        warm = keep.tile([P, 1], F32, name="warm")
        nc.gpsimd.memset(warm[:], 0.0)
        nc.scalar.activation(out=warm[:], in_=warm[:], func=ACT.Exp)

        nets = []
        stats = {}
        for power in ("e1", "e4"):
            stats[power] = gate.tile([P, TILES, 3], F32, name="stats_" + power)
        minus_cond, alpha = [], []
        complete = []
        waiting, issued = [], [0]
        x_sb, x_t, x_grouped, x_q = {}, {}, {}, {}
        planes, z, h_grouped, h_q, acc, logits, neg_max, e, e4, e_sum, beta = {}, {}, {}, {}, {}, {}, {}, {}, {}, {}, {}

        def run(stage, index, first, last):
            if first <= index < last:
                stage(index)

        def rows_of(k):
            return slice(PIECES[k][1] * P, PIECES[k][2] * P)

        def width(k):
            return (PIECES[k][2] - PIECES[k][1]) * P

        def net_of(k):
            return nets[PIECES[k][0] // GROUPS]

        def load_x(k):
            g, first, last = PIECES[k]
            x_sb[k] = three.tile([P, GROUP_TILES * D_IN], BF16, name="x_sb")
            nc.sync.dma_start(
                out=x_sb[k][:, : (last - first) * D_IN].rearrange("p (j k) -> p j k", j=last - first),
                in_=x_rows[:, g * GROUP_TILES + first : g * GROUP_TILES + last, :],
            )

        def transpose_x(k):
            x_words = x_sb[k][:].bitcast(F32)
            x_t[k] = []
            for pair in range(width(k) // (2 * P)):
                bank = psum_x.tile([P, 2, 2, P], F32, name="x_t")
                for jj in range(2):
                    for u in range(2):
                        start = (2 * pair + jj) * WORDS
                        nc.tensor.transpose(bank[:, jj, u, :], x_words[:, start + u : start + WORDS : 2], identity[:])
                x_t[k].append(bank)

        def copy_x_out(k, on_vector):
            if k not in x_grouped:
                x_grouped[k] = two.tile([P, GROUP_ROWS * PACK], BF16, name="x_grouped", align_bytes=64)
            grouped_words = x_grouped[k][:].bitcast(F32)
            for pair, bank in enumerate(x_t[k]):
                if ((k, pair) in VECTOR_X_BANKS) != on_vector:
                    continue
                out = grouped_words[:, pair * 2 * WORDS : (pair + 1) * 2 * WORDS].rearrange("p (j r u) -> p j r u", j=2, u=2)
                in_ = bank[:].rearrange("p j u r -> p j r u")
                if on_vector:
                    nc.vector.tensor_copy(out=out, in_=in_)
                else:
                    nc.scalar.copy(out=out, in_=in_)

        def quantise_x(k):
            g, first, last = PIECES[k]
            if first == 0:
                x_q[g] = (
                    keep.tile([P, GROUP_ROWS], U32, name="x_codes_%d" % g, align_bytes=64),
                    keep.tile([P, GROUP_ROWS], U8, name="x_scales_%d" % g, align_bytes=64),
                )
            quantise(nc, x_grouped[k][:, : width(k) * PACK], x_q[g][0][:, rows_of(k)], x_q[g][1][:, rows_of(k)])

        def hidden_product(k, t):
            if k < COUNT:
                codes, scales = net_of(k)["w1"]
                rows = x_q[PIECES[k][0] % GROUPS]
                z[(k, t)] = psum_z.tile([P, GROUP_ROWS], F32, name="z")
                cols = slice(t * P, (t + 1) * P)
                mx_pass(
                    nc,
                    z[(k, t)][:, : width(k)],
                    (codes[:, cols], scales[:, cols]),
                    (rows[0][:, rows_of(k)], rows[1][:, rows_of(k)]),
                )

        def hidden_layer(k):
            if 0 <= k < COUNT:
                planes[k] = three.tile([P, PACK, GROUP_ROWS], BF16, name="planes")
            for t in range(PACK):
                if t == 1 and k - 2 in TURNED:
                    turn_logits(k - 2)
                if 0 <= k < COUNT:
                    nc.scalar.activation(
                        out=planes[k][:, t, : width(k)],
                        in_=z[(k, t)][:, : width(k)],
                        func=ACT.Relu,
                        bias=net_of(k)["b1"][:, t : t + 1],
                        scale=1.0,
                    )
                hidden_product(k + 1, t)

        def regroup_h(k):
            h_grouped[k] = two.tile([P, GROUP_ROWS, PACK], BF16, name="h_grouped", align_bytes=64)
            rows = slice(0, GPSIMD_FROM + OVERLAP if k in GPSIMD_PIECES else width(k))
            nc.vector.tensor_copy(
                out=h_grouped[k][:, rows, :].rearrange("p (c i) t -> p c t i", i=4),
                in_=planes[k][:, :, rows].rearrange("p t (c i) -> p c t i", i=4),
            )
            if k in GPSIMD_PIECES:
                rows = slice(GPSIMD_FROM, GROUP_ROWS)
                nc.gpsimd.tensor_scalar(
                    out=h_grouped[k][:, rows, :],
                    in0=planes[k][:, :, rows].rearrange("p t r -> p r t"),
                    scalar1=1.0,
                    scalar2=0.0,
                    op0=ALU.mult,
                    op1=ALU.add,
                )

        def quantise_h(k):
            h_q[k] = (
                two.tile([P, GROUP_ROWS], U32, name="h_codes", align_bytes=64),
                two.tile([P, GROUP_ROWS], U8, name="h_scales", align_bytes=64),
            )
            n = width(k)
            quantise(nc, h_grouped[k][:, :n, :].rearrange("p r t -> p (r t)"), h_q[k][0][:, :n], h_q[k][1][:, :n])

        def head(k):
            w2 = net_of(k)["w2"]
            acc[k] = psum_l.tile([P, GROUP_TILES, CLASSES], F32, name="acc")
            if k in TURNED:
                n = width(k)
                out = acc[k][:].rearrange("p j r -> p (j r)")[:, :n]
                mx_pass(nc, out, (w2[0][:], w2[1][:]), (h_q[k][0][:, :n], h_q[k][1][:, :n]))
            else:
                for j in range(width(k) // P):
                    cols = slice(j * P, (j + 1) * P)
                    mx_pass(nc, acc[k][:, j, :], (h_q[k][0][:, cols], h_q[k][1][:, cols]), (w2[0][:], w2[1][:]))

        def add_bias(k):
            if k in TURNED:
                return
            n = width(k) // P
            logits[k] = three.tile([P, GROUP_TILES, CLASSES], F32, name="logits")
            nc.vector.tensor_tensor(
                out=logits[k][:, :n, :],
                in0=acc[k][:, :n, :],
                in1=net_of(k)["b2_row"][:].unsqueeze(1).to_broadcast([P, n, CLASSES]),
                op=ALU.add,
            )

        def turn_logits(k):
            class_rows = two.tile([P, GROUP_TILES, P], F32, name="class_rows")
            n = width(k) // P
            nc.scalar.activation(
                out=class_rows[:, :n, :],
                in_=acc[k][:, :n, :],
                func=ACT.Identity,
                bias=net_of(k)["b2_col"][:, 0:1],
                scale=1.0,
            )
            logits[k] = psum_x.tile([P, GROUP_TILES, CLASSES], F32, name="x_t")
            for j in range(n):
                nc.tensor.transpose(logits[k][:, j, :], class_rows[:, j, :], identity[:])

        def row_max(k):
            n = width(k) // P
            neg_max[k] = three.tile([P, GROUP_TILES], F32, name="neg_max")
            nc.vector.tensor_reduce(
                out=neg_max[k][:, :n], in_=logits[k][:, :n, :], axis=AXIS.X, op=ALU.max, negate=True
            )

        def exponentials(k):
            n = width(k) // P
            if k < O_COUNT:
                e[k] = keep.tile([P, n, CLASSES], F32, name="e_o_%d" % k)
                e4[k] = two.tile([P, GROUP_TILES, CLASSES], F32, name="e4")
                neg_max4 = two.tile([P, GROUP_TILES], F32, name="neg_max4")
                nc.scalar.activation(out=neg_max4[:, :n], in_=neg_max[k][:, :n], func=ACT.Copy, scale=4.0)
                for j in range(n):
                    nc.scalar.activation(
                        out=e[k][:, j, :], in_=logits[k][:, j, :], func=ACT.Exp, bias=neg_max[k][:, j : j + 1], scale=1.0
                    )
                for j in range(n):
                    nc.scalar.activation(
                        out=e4[k][:, j, :], in_=logits[k][:, j, :], func=ACT.Exp, bias=neg_max4[:, j : j + 1], scale=4.0
                    )
            else:
                e[k] = six.tile([P, GROUP_TILES, CLASSES], F32, name="e_f")
                if k not in SECOND:
                    e_sum[k] = four.tile([P, 2 * GROUP_TILES], F32, name="sum_f")
                sums = e_sum[k - 1][:, GROUP_TILES:] if k in SECOND else e_sum[k][:]
                for j in range(n):
                    nc.scalar.activation(
                        out=e[k][:, j, :],
                        in_=logits[k][:, j, :],
                        func=ACT.Exp,
                        bias=neg_max[k][:, j : j + 1],
                        scale=1.0,
                        accum_out=sums[:, j : j + 1],
                    )

        def sums_f(k):
            return e_sum[k], 2 * GROUP_TILES if k + 1 in SECOND else width(k) // P

        def statistics(k, power):
            g, first, last = PIECES[k]
            values = {"e1": e, "e4": e4}[power][k]
            for j in range(0, last - first, 2):
                tile = g * GROUP_TILES + first + j
                nc.vector.bn_stats(
                    out=stats[power][:, tile : tile + 2, :].rearrange("p j k -> p (j k)"),
                    in_=values[:, j : j + 2, :].rearrange("p j c -> p c j"),
                )

        def gate_half(half):
            slots, minus_cond_half, alpha_half = gate_slots(nc, gate, stats, half)
            waiting.extend(slots)
            complete.append(len(waiting))
            minus_cond.append(minus_cond_half)
            alpha.append(alpha_half)

        def gate_slot():
            if issued[0] < len(waiting):
                for instruction in waiting[issued[0]]:
                    instruction()
                issued[0] += 1

        def pieces_to_blend(turn):
            paired = range(O_COUNT, SECOND[-1] + 1)
            return [k for k in range(O_COUNT, COUNT) if turn == k + (4 if k in paired else 3)]

        def e_o(k, j):
            g, tile = PIECES[k][0] - GROUPS, PIECES[k][1] + j
            for other, (step, first, last) in enumerate(PIECES[:O_COUNT]):
                if step == g and first <= tile < last:
                    return e[other][:, tile - first, :]

        def blend_scale_o(k):
            g, first, last = PIECES[k]
            g -= GROUPS
            assert issued[0] >= complete[g // HALF_GROUPS]
            for j in range(last - first):
                column = (g % HALF_GROUPS) * GROUP_TILES + first + j
                factor = alpha[g // HALF_GROUPS][:, column : column + 1]
                if k in SCALAR_SCALED:
                    nc.scalar.activation(out=e_o(k, j), in_=e_o(k, j), func=ACT.Copy, scale=factor)
                else:
                    nc.vector.tensor_scalar(out=e_o(k, j), in0=e_o(k, j), scalar1=factor, scalar2=None, op0=ALU.mult)

        def blend_reciprocal(k):
            tile, columns = sums_f(k)
            reciprocal = four.tile([P, 2 * GROUP_TILES], F32, name="reciprocal")
            nc.vector.reciprocal(out=reciprocal[:, :columns], in_=tile[:, :columns])
            beta[k] = (reciprocal, columns)

        def blend_beta(k):
            g, first, last = PIECES[k]
            g -= GROUPS
            tile, columns = beta[k]
            column = (g % HALF_GROUPS) * GROUP_TILES + first
            nc.vector.scalar_tensor_tensor(
                out=tile[:, :columns],
                in0=tile[:, :columns],
                scalar=-float(CLASSES),
                in1=minus_cond[g // HALF_GROUPS][:, column : column + columns],
                op0=ALU.mult,
                op1=ALU.mult,
            )

        def blend_and_store(k):
            g, first, last = PIECES[k]
            if k in SECOND:
                factor = beta[k - 1][0][:, GROUP_TILES:]
            else:
                factor = beta[k][0][:]
            for j in range(last - first):
                nc.vector.scalar_tensor_tensor(
                    out=e[k][:, j, :],
                    in0=e[k][:, j, :],
                    scalar=factor[:, j : j + 1],
                    in1=e_o(k, j),
                    op0=ALU.mult,
                    op1=ALU.add,
                )
            tiles = slice((g - GROUPS) * GROUP_TILES + first, (g - GROUPS) * GROUP_TILES + last)
            nc.sync.dma_start(out=out_rows[:, tiles, :], in_=e[k][:, : last - first, :])

        nets.extend([network_tiles(keep, "o"), network_tiles(keep, "f")])
        load_x(0)
        load_first(nc, nets[0], W1o, b1o)
        load_x(1)
        load_w2(nc, nets[0], W2o)
        nc.sync.dma_start(out=b2_first_row[0:1, 0:CLASSES], in_=b2o.rearrange("(o c) -> o c", o=1))
        nc.sync.dma_start(out=b2_first_row[0:1, CLASSES:], in_=b2f.rearrange("(o c) -> o c", o=1))
        load_x(2)
        load_first(nc, nets[1], W1f, b1f)
        load_w2(nc, nets[1], W2f)

        for i in range(-5, COUNT + 4):
            run(load_x, i + 5, 3, O_COUNT)
            early = i < O_COUNT
            if not early:
                run(regroup_h, i, 0, COUNT)
                gate_slot()
            if i == -3:
                lay_out_w1(nc, nets[0], 0)
                lay_out_w1(nc, nets[0], 1)
                quantise_w1(nc, nets[0], 0, PACK // 2)
            run(quantise_x, i + 2, 0, O_COUNT)
            if i == -2:
                quantise_w1(nc, nets[0], PACK // 2, PACK)
            if early:
                if i + 2 < O_COUNT:
                    gate_slot()
                run(regroup_h, i, 0, COUNT)
                run(lambda k: statistics(k, "e1"), i - 3, 0, O_COUNT)
                run(add_bias, i - 1, 0, COUNT)
            run(hidden_layer, i + 1, -1, COUNT + 2)
            run(lambda k: copy_x_out(k, False), i + 3, 0, O_COUNT)
            run(lambda k: copy_x_out(k, True), i + 3, 0, O_COUNT)
            if i == -3:
                lay_out_b1(nc, nets[0])
            if i == -1:
                lay_out_w2(nc, nets[0])
            if i == 0:
                quantise_w2(nc, nets[0])
            if not early:
                run(lambda k: statistics(k, "e1"), i - 3, 0, O_COUNT)
            if early:
                run(lambda k: statistics(k, "e4"), i - 3, 0, O_COUNT)
                run(row_max, i - 1, 0, COUNT)
            due = pieces_to_blend(i)
            for k in due:
                if k not in SECOND:
                    blend_reciprocal(k)
            if not early:
                run(add_bias, i - 1, 0, COUNT)
                if i - 3 not in SCALAR_SCALED:
                    run(blend_scale_o, i - 3, O_COUNT, COUNT)
            gate_slot()
            run(quantise_h, i, 0, COUNT)
            gate_slot()
            run(transpose_x, i + 4, 0, O_COUNT)
            run(head, i, 0, COUNT)
            if not early:
                run(lambda k: statistics(k, "e4"), i - 3, 0, O_COUNT)
                for k in due:
                    if k not in SECOND:
                        blend_beta(k)
                run(row_max, i - 1, 0, COUNT)
                gate_slot()
            if i - 3 in SCALAR_SCALED:
                blend_scale_o(i - 3)
            run(exponentials, i - 2, 0, COUNT)
            for k in due:
                blend_and_store(k)
            if i == 1 or i == 2:
                lay_out_w1(nc, nets[1], i - 1)
            if i == -2:
                b2_spread = psum_l.tile([P, GROUP_TILES, CLASSES], F32, name="acc")
                for n in range(2):
                    row = b2_first_row[:, n * CLASSES : (n + 1) * CLASSES]
                    nc.tensor.matmul(out=b2_spread[:, n, :], lhsT=ones[:], rhs=row, start=True, stop=True)
                    nc.tensor.matmul(out=b2_spread[:, 2 + n, :], lhsT=row, rhs=ones[:], start=True, stop=True)
            if i == -1:
                for n in range(2):
                    copy_on(nc, "scalar", nets[n]["b2_row"][:], b2_spread[:, n, :])
                copy_on(nc, "scalar", nets[1]["b2_col"][:], b2_spread[:, 3, 0:1])
            if i == 2:
                lay_out_b1(nc, nets[1])
                lay_out_w2(nc, nets[1])
            if i == 4:
                quantise_w1(nc, nets[1], 0, PACK)
                quantise_w2(nc, nets[1])
            if i - 3 in (HALF_GROUPS, O_COUNT - 1):
                assert issued[0] == len(waiting)
                gate_half((i - 3) // HALF_GROUPS - 1)
